import numpy as np
import ml_dtypes


def mxq(x, axis, fmt="e4m3"):
    dtype, down = {"e4m3": (ml_dtypes.float8_e4m3fn, 7), "e5m2": (ml_dtypes.float8_e5m2, 14)}[fmt]
    v = np.moveaxis(np.asarray(x, np.float32).astype(ml_dtypes.bfloat16).astype(np.float64), axis, -1)
    blocks = v.reshape(v.shape[:-1] + (-1, 32))
    amax = np.abs(blocks).max(-1, keepdims=True)
    byte = np.maximum(np.where(amax > 0, np.frexp(amax)[1] - 1 + 127, 0) - down, 1)
    scale = np.exp2(byte - 127.0)
    codes = (blocks / scale).astype(np.float32).astype(dtype).astype(np.float64)
    return np.moveaxis((codes * scale).reshape(v.shape), -1, axis)


WIDE = False


def mx_kscale(k):
    if not WIDE:
        return np.ones(k)
    levels = np.array([10, -10, 5, -5, 0])
    a = np.random.permutation(np.resize(levels, k // 512 * 4)).reshape(k // 512, 4)
    idx = np.arange(k)
    return np.exp2(a[idx // 512, idx % 128 // 32])


BF16 = ml_dtypes.bfloat16


def bf(x):
    return np.asarray(x, np.float32).astype(BF16)


def f64(x):
    return np.asarray(x).astype(np.float64)


B, N, D, H, HD, S, DO = 1, 1536, 1024, 16, 64, 11, 1024
E = H * HD
D4 = [0.4829629131445341, 0.8365163037378079, 0.2241438680420134, -0.1294095225512604]
T = len(D4)


def elu1(u):
    return np.where(u > 0.0, u, np.exp(np.minimum(u, 0.0)) - 1.0) + 1.0


def softplus(u):
    return np.log(1.0 + np.exp(u))


def shifted(t, o):
    if o == 0:
        return t
    return np.concatenate([np.zeros((B, H, o, HD)), t[:, :, :N - o, :]], axis=2)


def setup_inputs():
    s = mx_kscale(D)
    lg = np.random.standard_normal((B, H, N, S)) * 1.4
    g = np.exp(lg - lg.max(-1, keepdims=True))
    return {"x": bf(np.random.standard_normal((B, N, D)) * s),
            "W_qkv": bf(np.random.standard_normal((3 * E, D)) * 0.6 / np.sqrt(D) / s),
            "b_qkv": bf(np.random.standard_normal(3 * E) * 0.1),
            "gains": bf(g / g.sum(-1, keepdims=True)),
            "pos_bias": bf(np.random.standard_normal((S * T, H)) * 0.5),
            "identity_bypass": bf(-1.0 + 0.5 * np.random.standard_normal(H))}


def reference(x, W_qkv, b_qkv, gains, pos_bias, identity_bypass):
    qkv = (mxq(f64(x), 2, "e4m3") @ mxq(f64(W_qkv), 1, "e4m3").T) + f64(b_qkv)
    q, k, v = [t.reshape(B, N, H, HD).transpose(0, 2, 1, 3) for t in np.split(qkv, 3, axis=-1)]
    g, pb = f64(gains), f64(pos_bias)
    acc = np.zeros((B, H, N, HD))
    z = np.zeros((B, H, N, 1))
    tap = 0
    for j in range(S):
        d = 1 << j
        g_j = g[..., j][..., None]
        for tau, c in enumerate(D4):
            o = d * tau
            bias = pb[tap].reshape(1, H, 1, 1)
            tap += 1
            if o != 0 and o >= N:
                continue
            k_s, v_s = shifted(k, o), shifted(v, o)
            feat = elu1(np.sum(q * k_s, -1, keepdims=True) + bias)
            acc = acc + (g_j * c) * feat * v_s
            z = z + g_j * abs(c) * feat
    p = softplus(f64(identity_bypass)).reshape(1, H, 1, 1)
    local = elu1(np.sum(q * k, -1, keepdims=True))
    acc = acc + p * local * v
    z = z + p * local
    res = acc / (z + 1e-06)
    return res.transpose(0, 2, 1, 3).reshape(B, N, E)

@@ -1,0 +1,434 @@
+from contextlib import ExitStack
+
+import concourse.mybir as mybir
+from concourse.masks import make_identity
+
+F32 = mybir.dt.float32
+BF16 = mybir.dt.bfloat16
+U32 = mybir.dt.uint32
+U8 = mybir.dt.uint8
+FP8X4 = mybir.dt.float8_e4m3fn_x4
+ALU = mybir.AluOpType
+ACT = mybir.ActivationFunctionType
+AXIS = mybir.AxisListType
+
+P = 128
+TOKENS = 1536
+TILES = TOKENS // P
+D_IN = 1024
+HEADS = 16
+HEAD_DIM = 64
+E = HEADS * HEAD_DIM
+PACK = 4
+PASSES = D_IN // (P * PACK)
+BANK = 512
+BLOCKS = BANK // P
+GROUPS = 8
+PAD = P
+
+D4 = [0.4829629131445341, 0.8365163037378079, 0.2241438680420134, -0.1294095225512604]
+SCALES = 11
+
+POW_SLOT = 1
+TRI_SLOT = 12
+OFFSETS = [0] + [1 << e for e in range(11)] + [3 << j for j in range(9)]
+SLOTS = len(OFFSETS)
+BAND = 128
+NEAR_SLOTS = [s for s in range(SLOTS) if OFFSETS[s] <= BAND]
+FAR_SLOTS = [s for s in range(SLOTS) if OFFSETS[s] > BAND]
+
+LOCAL = 11
+TAU1 = 12
+TAU2 = 23
+TAU3 = 34
+ENTRIES = 43
+
+HEAD_SETS = 4
+SET = HEADS // HEAD_SETS
+PITCH = 2 * P
+
+FLOPS = 2 * TOKENS * D_IN * 3 * E + 4 * TOKENS * E * 42
+
+
+def runs_of_slots(slots, longest):
+    runs = []
+    for s in slots:
+        if runs and runs[-1][-1] == s - 1 and len(runs[-1]) < longest:
+            runs[-1].append(s)
+        else:
+            runs.append([s])
+    return runs
+
+
+def tile_dwarfattention_pa_kernel(tc, x, W_qkv, b_qkv, gains, pos_bias, identity_bypass, out):
+    nc = tc.nc
+    out_rows = out.rearrange("o n f -> (o n) f")
+    out_words = out.rearrange("o n f -> (o n f)")
+
+    with ExitStack() as whole:
+        const = whole.enter_context(tc.tile_pool(name="const", bufs=1))
+        keep = whole.enter_context(tc.tile_pool(name="keep", bufs=1))
+
+        ident = const.tile([P, P], F32, name="ident")
+        make_identity(nc, ident[:])
+
+        q_feat = keep.tile([P, GROUPS, TOKENS], F32, name="q_feat")
+        k_feat = keep.tile([P, GROUPS, PAD + TOKENS], F32, name="k_feat")
+        nc.vector.memset(k_feat[:, :, 0:PAD], 0.0)
+
+        bias_qk_bf = const.tile([P, 2, GROUPS], BF16, name="bias_qk_bf")
+        nc.scalar.dma_start(out=bias_qk_bf[:], in_=b_qkv.rearrange("(s r a) -> r s a", s=3, a=GROUPS)[:, 0:2, :])
+        bias_qk = const.tile([P, 2, GROUPS], F32, name="bias_qk")
+        nc.vector.tensor_copy(out=bias_qk[:], in_=bias_qk_bf[:])
+
+        pos_bf = const.tile([P, SCALES, 4, HEADS], BF16, name="pos_bf")
+        nc.scalar.dma_start(
+            out=pos_bf[:].rearrange("p j t h -> p (j t h)"),
+            in_=pos_bias.rearrange("r h -> (r h)").partition_broadcast(P),
+        )
+        bypass_bf = const.tile([P, HEADS], BF16, name="bypass_bf")
+        nc.scalar.dma_start(out=bypass_bf[:], in_=identity_bypass.partition_broadcast(P))
+        gains_sb = const.tile([P, HEADS, TILES, SCALES], BF16, name="gains_sb")
+        nc.scalar.dma_start(
+            out=gains_sb[:].rearrange("p h t j -> p (h t) j"),
+            in_=gains.rearrange("o h (t p) j -> p (o h t) j", p=P),
+        )
+
+        bias_plus_1 = const.tile([P, ENTRIES, HEADS], F32, name="bias_plus_1")
+        nc.vector.memset(bias_plus_1[:], 1.0)
+        for first, tau, j_count in ((0, 0, 11), (TAU1, 1, 11), (TAU2 + 1, 2, 10), (TAU3, 3, 9)):
+            nc.vector.tensor_scalar_add(
+                out=bias_plus_1[:, first : first + j_count, :], in0=pos_bf[:, 0:j_count, tau, :], scalar1=1.0
+            )
+
+        soft = const.tile([P, 3, HEADS], F32, name="soft")
+        nc.scalar.activation(out=soft[:, 0, :], in_=bypass_bf[:], func=ACT.Abs)
+        nc.scalar.activation(out=soft[:, 1, :], in_=soft[:, 0, :], func=ACT.Exp, scale=-1.0)
+        nc.scalar.activation(out=soft[:, 2, :], in_=soft[:, 1, :], func=ACT.Ln, bias=1.0)
+        nc.vector.tensor_scalar_max(out=soft[:, 0, :], in0=bypass_bf[:], scalar1=0.0)
+        tap_gains = []
+        for turn in range(2):
+            tap_gain = const.tile([P, ENTRIES, HEADS], F32, name="tap_gain%d" % turn)
+            nc.vector.memset(tap_gain[:, TAU2, :], 0.0)
+            nc.vector.tensor_tensor(out=tap_gain[:, LOCAL, :], in0=soft[:, 0, :], in1=soft[:, 2, :], op=ALU.add)
+            tap_gains.append(tap_gain)
+
+        with ExitStack() as phase:
+            raw_pool = phase.enter_context(tc.tile_pool(name="raw", bufs=3))
+            grouped_pool = phase.enter_context(tc.tile_pool(name="grouped", bufs=2))
+            x_pool = phase.enter_context(tc.tile_pool(name="x_mx", bufs=1))
+            w_pool = phase.enter_context(tc.tile_pool(name="w_mx", bufs=2))
+            v_pool = phase.enter_context(tc.tile_pool(name="v_stage", bufs=3))
+            turned_psum = phase.enter_context(tc.psum_pool(name="turned", bufs=4))
+            acc_psum = phase.enter_context(tc.psum_pool(name="acc", bufs=4))
+
+            bias_v_bf = v_pool.tile([P, E], BF16, name="bias_v_bf", bufs=1)
+            nc.scalar.dma_start(out=bias_v_bf[:], in_=b_qkv[2 * E : 3 * E].partition_broadcast(P))
+            bias_v = v_pool.tile([P, E], F32, name="bias_v", bufs=1)
+            nc.vector.tensor_copy(out=bias_v[:], in_=bias_v_bf[:])
+
+            def quantise_512_rows(rows, codes, scales):
+                raw = raw_pool.tile([P, BLOCKS, D_IN], BF16, name="raw")
+                nc.sync.dma_start(out=raw[:], in_=rows)
+                grouped = grouped_pool.tile([P, PASSES, BANK * PACK], BF16, name="grouped", align_bytes=64)
+                grouped_words = grouped[:].bitcast(F32).rearrange("p g (c u) -> p g c u", u=2)
+                for c in range(BLOCKS):
+                    raw_words = raw[:, c, :].bitcast(F32)
+                    turned = turned_psum.tile([P, PASSES, 2, P], F32, name="turned")
+                    for g in range(PASSES):
+                        for u in range(2):
+                            first = (2 * g + u) * P
+                            nc.tensor.transpose(turned[:, g, u, :], raw_words[:, first : first + P], ident[:])
+                    dst = grouped_words[:, :, c * P : (c + 1) * P, :]
+                    src = turned[:].rearrange("p g u c -> p g c u")
+                    if c % 2 == 0:
+                        nc.vector.tensor_copy(out=dst, in_=src)
+                    else:
+                        nc.scalar.copy(out=dst, in_=src)
+                for g in range(PASSES):
+                    nc.vector.quantize_mx(out=codes[:, g, :].bitcast(FP8X4), scales=scales[:, g, :], in_=grouped[:, g, :])
+
+            x_codes = x_pool.tile([P, PASSES, TOKENS], U32, name="x_codes", align_bytes=64)
+            x_scales = x_pool.tile([P, PASSES, TOKENS], U8, name="x_scales", align_bytes=64)
+            x_blocks = x.rearrange("o (n c p) k -> (o n) p c k", c=BLOCKS, p=P)
+            for n in range(TOKENS // BANK):
+                cols = slice(n * BANK, (n + 1) * BANK)
+                quantise_512_rows(x_blocks[n], x_codes[:, :, cols], x_scales[:, :, cols])
+
+            def quantise_third(row_views):
+                w_codes = w_pool.tile([P, PASSES, E], U32, name="w_codes", align_bytes=64)
+                w_scales = w_pool.tile([P, PASSES, E], U8, name="w_scales", align_bytes=64)
+                for n, rows in enumerate(row_views):
+                    cols = slice(n * BANK, (n + 1) * BANK)
+                    quantise_512_rows(rows, w_codes[:, :, cols], w_scales[:, :, cols])
+                return w_codes, w_scales
+
+            w_by_group = W_qkv.rearrange("(s r a) k -> s r a k", s=3, a=GROUPS)
+            for third, dest, pad in ((0, q_feat, 0), (1, k_feat, PAD)):
+                w_codes, w_scales = quantise_third(
+                    [w_by_group[third][:, n * BLOCKS : (n + 1) * BLOCKS, :] for n in range(E // BANK)]
+                )
+                for a in range(GROUPS):
+                    feats = slice(a * P, (a + 1) * P)
+                    for n in range(TOKENS // BANK):
+                        toks = slice(n * BANK, (n + 1) * BANK)
+                        acc = acc_psum.tile([P, BANK], F32, name="acc")
+                        for g in range(PASSES):
+                            nc.tensor.matmul_mx(
+                                out=acc[:],
+                                lhsT=w_codes[:, g, feats].bitcast(FP8X4),
+                                lhsT_scale=w_scales[:, g, feats],
+                                rhs=x_codes[:, g, toks].bitcast(FP8X4),
+                                rhs_scale=x_scales[:, g, toks],
+                                start=(g == 0),
+                                stop=(g == PASSES - 1),
+                            )
+                        dst = dest[:, a, pad + n * BANK : pad + (n + 1) * BANK]
+                        bias = bias_qk[:, third, a : a + 1]
+                        if n % 2 == 0:
+                            nc.scalar.activation(out=dst, in_=acc[:], func=ACT.Identity, bias=bias)
+                        else:
+                            nc.vector.tensor_scalar_add(out=dst, in0=acc[:], scalar1=bias)
+
+            w_natural = W_qkv.rearrange("(s n c p) k -> s n p c k", s=3, c=BLOCKS, p=P)
+            w_codes, w_scales = quantise_third([w_natural[2][n] for n in range(E // BANK)])
+            for t in range(TILES):
+                toks = slice(t * P, (t + 1) * P)
+                v_stage = v_pool.tile([P, E], F32, name="v_stage")
+                for n in range(E // BANK):
+                    feats = slice(n * BANK, (n + 1) * BANK)
+                    acc = acc_psum.tile([P, BANK], F32, name="acc")
+                    for g in range(PASSES):
+                        nc.tensor.matmul_mx(
+                            out=acc[:],
+                            lhsT=x_codes[:, g, toks].bitcast(FP8X4),
+                            lhsT_scale=x_scales[:, g, toks],
+                            rhs=w_codes[:, g, feats].bitcast(FP8X4),
+                            rhs_scale=w_scales[:, g, feats],
+                            start=(g == 0),
+                            stop=(g == PASSES - 1),
+                        )
+                    nc.vector.tensor_tensor(out=v_stage[:, feats], in0=acc[:], in1=bias_v[:, feats], op=ALU.add)
+                nc.sync.dma_start(out=out_rows[toks, :], in_=v_stage[:])
+
+        with ExitStack() as phase:
+            prod_pool = phase.enter_context(tc.tile_pool(name="prod", bufs=3))
+            mid_pool = phase.enter_context(tc.tile_pool(name="mid", bufs=1))
+            lag_pool = phase.enter_context(tc.tile_pool(name="lag", bufs=2))
+            band_pool = phase.enter_context(tc.tile_pool(name="band", bufs=2 * HEAD_SETS))
+            bandT_pool = phase.enter_context(tc.tile_pool(name="bandT", bufs=4))
+            near_pool = phase.enter_context(tc.tile_pool(name="v_near", bufs=2))
+            far_pool = phase.enter_context(tc.tile_pool(name="v_far", bufs=len(FAR_SLOTS)))
+            score_psum = phase.enter_context(tc.psum_pool(name="score", bufs=2))
+            bandT_psum = phase.enter_context(tc.psum_pool(name="bandT_ps", bufs=2))
+            sum_psum = phase.enter_context(tc.psum_pool(name="sum", bufs=1))
+
+            band_rows = mid_pool.tile([P, HEADS, PITCH], F32, name="band_rows")
+            nc.vector.memset(band_rows[:], 0.0)
+
+            def load_v_tile(t):
+                v_near = near_pool.tile([P, E], F32, name="v_near")
+                nc.sync.dma_start(out=v_near[:], in_=out_rows[t * P : (t + 1) * P, :])
+                return v_near
+
+            def scores(t):
+                score = lag_pool.tile([P, SLOTS, HEADS], F32, name="score")
+                live = [s for s in range(SLOTS) if OFFSETS[s] < (t + 1) * P]
+                if len(live) < SLOTS:
+                    nc.vector.memset(score[:], 0.0)
+                for run in runs_of_slots(live, BLOCKS):
+                    partial = score_psum.tile([P, BLOCKS, P], F32, name="partial")
+                    for i, s in enumerate(run):
+                        first = PAD + t * P - OFFSETS[s]
+                        prod = prod_pool.tile([P, GROUPS, P], F32, name="prod")
+                        nc.vector.tensor_tensor(
+                            out=prod[:],
+                            in0=q_feat[:, :, t * P : (t + 1) * P],
+                            in1=k_feat[:, :, first : first + P],
+                            op=ALU.mult,
+                        )
+                        for a in range(GROUPS):
+                            nc.tensor.matmul(
+                                out=partial[:, i, :],
+                                lhsT=prod[:, a, :],
+                                rhs=ident[:],
+                                is_transpose=True,
+                                start=(a == 0),
+                                stop=(a == GROUPS - 1),
+                            )
+                    nc.vector.tensor_reduce(
+                        out=score[:, run[0] : run[0] + len(run), :],
+                        in_=partial[:, 0 : len(run), :].rearrange("p s (h b) -> p s h b", b=GROUPS),
+                        axis=AXIS.X,
+                        op=ALU.add,
+                    )
+                return score
+
+            def weights(t, score, tap_gain):
+                g_jh = gains_sb[:, :, t, :].rearrange("p h j -> p j h")
+                nc.scalar.mul(out=tap_gain[:, 0:11, :], in_=g_jh, mul=D4[0])
+                nc.scalar.mul(out=tap_gain[:, TAU1 : TAU1 + 11, :], in_=g_jh, mul=D4[1])
+                nc.scalar.mul(out=tap_gain[:, TAU2 + 1 : TAU2 + 11, :], in_=g_jh[:, 0:10, :], mul=D4[2])
+                nc.scalar.mul(out=tap_gain[:, TAU3 : TAU3 + 9, :], in_=g_jh[:, 0:9, :], mul=abs(D4[3]))
+
+                u_plus_1 = mid_pool.tile([P, ENTRIES, HEADS], F32, name="u_plus_1")
+                nc.vector.tensor_tensor(
+                    out=u_plus_1[:, 0:TAU1, :],
+                    in0=score[:, 0:1, :].to_broadcast([P, TAU1, HEADS]),
+                    in1=bias_plus_1[:, 0:TAU1, :],
+                    op=ALU.add,
+                )
+                nc.vector.tensor_tensor(
+                    out=u_plus_1[:, TAU1:TAU3, :].rearrange("p (b s) h -> p b (s h)", b=2),
+                    in0=score[:, POW_SLOT:TRI_SLOT, :]
+                    .rearrange("p s h -> p (s h)")
+                    .unsqueeze(1)
+                    .to_broadcast([P, 2, 11 * HEADS]),
+                    in1=bias_plus_1[:, TAU1:TAU3, :].rearrange("p (b s) h -> p b (s h)", b=2),
+                    op=ALU.add,
+                )
+                nc.vector.tensor_tensor(
+                    out=u_plus_1[:, TAU3:ENTRIES, :],
+                    in0=score[:, TRI_SLOT:SLOTS, :],
+                    in1=bias_plus_1[:, TAU3:ENTRIES, :],
+                    op=ALU.add,
+                )
+                feat = mid_pool.tile([P, ENTRIES, HEADS], F32, name="feat")
+                feat_flat = feat[:].rearrange("p e h -> p (e h)")
+                u_flat = u_plus_1[:].rearrange("p e h -> p (e h)")
+                nc.scalar.activation(out=feat_flat, in_=u_flat, func=ACT.Exp, bias=-1.0)
+                nc.vector.scalar_tensor_tensor(
+                    out=feat_flat, in0=feat_flat, scalar=1.0, in1=u_flat, op0=ALU.min, op1=ALU.max
+                )
+                tap_mass = mid_pool.tile([P, TAU3, HEADS], F32, name="tap_mass")
+                mass = mid_pool.tile([P, SLOTS, HEADS], F32, name="mass")
+                nc.vector.tensor_tensor(out=tap_mass[:], in0=feat[:, 0:TAU3, :], in1=tap_gain[:, 0:TAU3, :], op=ALU.mult)
+                nc.vector.tensor_tensor(
+                    out=mass[:, TRI_SLOT:SLOTS, :], in0=feat[:, TAU3:ENTRIES, :], in1=tap_gain[:, TAU3:ENTRIES, :], op=ALU.mult
+                )
+                nc.vector.tensor_reduce(
+                    out=mass[:, 0, :], in_=tap_mass[:, 0:TAU1, :].rearrange("p e h -> p h e"), axis=AXIS.X, op=ALU.add
+                )
+                nc.vector.tensor_tensor(
+                    out=mass[:, POW_SLOT:TRI_SLOT, :], in0=tap_mass[:, TAU1:TAU2, :], in1=tap_mass[:, TAU2:TAU3, :], op=ALU.add
+                )
+                z = mid_pool.tile([P, HEADS], F32, name="z")
+                nc.vector.tensor_reduce(out=z[:], in_=mass[:].rearrange("p s h -> p h s"), axis=AXIS.X, op=ALU.add)
+                nc.vector.tensor_scalar_add(out=z[:], in0=z[:], scalar1=1e-6)
+                nc.vector.reciprocal(out=z[:], in_=z[:])
+                weight = lag_pool.tile([P, SLOTS, HEADS], F32, name="weight")
+                nc.vector.tensor_tensor(
+                    out=weight[:, 0:TRI_SLOT, :],
+                    in0=mass[:, 0:TRI_SLOT, :],
+                    in1=z[:].unsqueeze(1).to_broadcast([P, TRI_SLOT, HEADS]),
+                    op=ALU.mult,
+                )
+                nc.vector.scalar_tensor_tensor(
+                    out=weight[:, TRI_SLOT:SLOTS, :],
+                    in0=mass[:, TRI_SLOT:SLOTS, :],
+                    scalar=-1.0,
+                    in1=z[:].unsqueeze(1).to_broadcast([P, SLOTS - TRI_SLOT, HEADS]),
+                    op0=ALU.mult,
+                    op1=ALU.mult,
+                )
+                return weight
+
+            def skew(t, weight):
+                for s in NEAR_SLOTS:
+                    nc.scalar.copy(out=band_rows[:, :, BAND - OFFSETS[s]], in_=weight[:, s, :])
+                free_tiles = [t, t + 1] if t + 1 < TILES else [t]
+                key_tiles = [0, 1] if t > 0 else [1]
+                bands = []
+                for first in range(0, HEAD_SETS, len(free_tiles)):
+                    places = [(first + i, out_words[r * P * E : (r + 1) * P * E]) for i, r in enumerate(free_tiles)]
+                    for hs, words in places:
+                        nc.sync.dma_start(
+                            out=words.rearrange("(h n c) -> n h c", h=SET, c=PITCH),
+                            in_=band_rows[:, hs * SET : (hs + 1) * SET, :],
+                        )
+                    for hs, words in places:
+                        by_head = words.rearrange("(h w) -> h w", h=SET)
+                        band = {}
+                        for kt in key_tiles:
+                            band[kt] = band_pool.tile([P, SET, P], F32, name="band")
+                            nc.sync.dma_start(
+                                out=band[kt][:],
+                                in_=by_head[:, kt * P : kt * P + P * (PITCH - 1)].rearrange(
+                                    "h (n c) -> n h c", c=PITCH - 1
+                                )[:, :, 0:P],
+                            )
+                        bands.append(band)
+                return bands
+
+            def load_far(t):
+                tiles = []
+                for s in FAR_SLOTS:
+                    first = t * P - OFFSETS[s]
+                    if first + P <= 0:
+                        continue
+                    v_far = far_pool.tile([P, E], F32, name="v_far")
+                    missing = max(0, -first)
+                    if missing:
+                        nc.vector.memset(v_far[0:missing, :], 0.0)
+                    nc.sync.dma_start(out=v_far[missing:P, :], in_=out_rows[first + missing : first + P, :])
+                    tiles.append((s, v_far))
+                return tiles
+
+            def weighted_sums(t, weight, bands, v_near, v_far):
+                key_tiles = [0, 1] if t > 0 else [1]
+                sums = [sum_psum.tile([P, BANK], F32, name="sum%d" % i) for i in range(E // BANK)]
+                for hs in range(HEAD_SETS):
+                    bandT = {}
+                    for kt in key_tiles:
+                        bandT_ps = bandT_psum.tile([P, SET, P], F32, name="bandT_ps")
+                        for i in range(SET):
+                            nc.tensor.transpose(bandT_ps[:, i, :], bands[hs][kt][:, i, :], ident[:])
+                        bandT[kt] = bandT_pool.tile([P, SET, P], F32, name="bandT")
+                        nc.scalar.copy(out=bandT[kt][:], in_=bandT_ps[:])
+                    for i in range(SET):
+                        h = hs * SET + i
+                        for kt in key_tiles:
+                            nc.tensor.matmul(
+                                out=sums[h * HEAD_DIM // BANK][:, h * HEAD_DIM % BANK : h * HEAD_DIM % BANK + HEAD_DIM],
+                                lhsT=bandT[kt][:, i, :],
+                                rhs=v_near[t - 1 + kt][:, h * HEAD_DIM : (h + 1) * HEAD_DIM],
+                                start=(kt == key_tiles[0]),
+                                stop=(kt == key_tiles[-1]),
+                            )
+                result = lag_pool.tile([P, E], F32, name="result")
+                if not v_far:
+                    for i in range(E // BANK):
+                        nc.vector.tensor_copy(out=result[:, i * BANK : (i + 1) * BANK], in_=sums[i][:])
+                for count, (s, v_o) in enumerate(v_far):
+                    for h in range(HEADS):
+                        cols = slice(h * HEAD_DIM, (h + 1) * HEAD_DIM)
+                        so_far = result[:, cols]
+                        if count == 0:
+                            so_far = sums[h * HEAD_DIM // BANK][:, h * HEAD_DIM % BANK : h * HEAD_DIM % BANK + HEAD_DIM]
+                        nc.vector.scalar_tensor_tensor(
+                            out=result[:, cols],
+                            in0=v_o[:, cols],
+                            scalar=weight[:, s, h : h + 1],
+                            in1=so_far,
+                            op0=ALU.mult,
+                            op1=ALU.add,
+                        )
+                return result
+
+            def store(t, result):
+                nc.sync.dma_start(out=out_rows[t * P : (t + 1) * P, :], in_=result[:])
+
+            v_near = {TILES - 1: load_v_tile(TILES - 1)}
+            waiting = None
+            for step, t in enumerate(reversed(range(TILES))):
+                weight = weights(t, scores(t), tap_gains[step % 2])
+                if waiting is not None:
+                    result = weighted_sums(*waiting)
+                bands = skew(t, weight)
+                if waiting is not None:
+                    store(t + 1, result)
+                v_far = load_far(t)
+                if t > 0:
+                    v_near[t - 1] = load_v_tile(t - 1)
+                waiting = (t, weight, bands, v_near, v_far)
+            store(0, weighted_sums(*waiting))

@@ -46,6 +46,9 @@ ENTRIES = 43
 HEAD_SETS = 4
 SET = HEADS // HEAD_SETS
 PITCH = 2 * P
+LAG = 2
+BAND_START = 8
+BAND_PACE = 2
 
 FLOPS = 2 * TOKENS * D_IN * 3 * E + 4 * TOKENS * E * 42
 
@@ -89,10 +92,6 @@ def tile_dwarfattention_pa_kernel(tc, x, W_qkv, b_qkv, gains, pos_bias, identity
         bypass_bf = const.tile([P, HEADS], BF16, name="bypass_bf")
         nc.scalar.dma_start(out=bypass_bf[:], in_=identity_bypass.partition_broadcast(P))
         gains_sb = const.tile([P, HEADS, TILES, SCALES], BF16, name="gains_sb")
-        nc.scalar.dma_start(
-            out=gains_sb[:].rearrange("p h t j -> p (h t) j"),
-            in_=gains.rearrange("o h (t p) j -> p (o h t) j", p=P),
-        )
 
         bias_plus_1 = const.tile([P, ENTRIES, HEADS], F32, name="bias_plus_1")
         nc.vector.memset(bias_plus_1[:], 1.0)
@@ -192,6 +191,10 @@ def tile_dwarfattention_pa_kernel(tc, x, W_qkv, b_qkv, gains, pos_bias, identity
 
             w_natural = W_qkv.rearrange("(s n c p) k -> s n p c k", s=3, c=BLOCKS, p=P)
             w_codes, w_scales = quantise_third([w_natural[2][n] for n in range(E // BANK)])
+            nc.sync.dma_start(
+                out=gains_sb[:].rearrange("p h t j -> p (h t) j"),
+                in_=gains.rearrange("o h (t p) j -> p (o h t) j", p=P),
+            )
             for t in range(TILES):
                 toks = slice(t * P, (t + 1) * P)
                 v_stage = v_pool.tile([P, E], F32, name="v_stage")
@@ -212,7 +215,7 @@ def tile_dwarfattention_pa_kernel(tc, x, W_qkv, b_qkv, gains, pos_bias, identity
                 nc.sync.dma_start(out=out_rows[toks, :], in_=v_stage[:])
 
         with ExitStack() as phase:
-            prod_pool = phase.enter_context(tc.tile_pool(name="prod", bufs=3))
+            prod_pool = phase.enter_context(tc.tile_pool(name="prod", bufs=4))
             mid_pool = phase.enter_context(tc.tile_pool(name="mid", bufs=1))
             lag_pool = phase.enter_context(tc.tile_pool(name="lag", bufs=2))
             band_pool = phase.enter_context(tc.tile_pool(name="band", bufs=2 * HEAD_SETS))
@@ -231,11 +234,52 @@ def tile_dwarfattention_pa_kernel(tc, x, W_qkv, b_qkv, gains, pos_bias, identity
                 nc.sync.dma_start(out=v_near[:], in_=out_rows[t * P : (t + 1) * P, :])
                 return v_near
 
-            def scores(t):
+            def sum_cols(job, h):
+                first = h * HEAD_DIM % BANK
+                return job["sums"][h * HEAD_DIM // BANK][:, first : first + HEAD_DIM]
+
+            def band_steps(job, count):
+                for i in range(job["steps_done"], min(job["steps_done"] + count, HEADS + LAG)):
+                    band_step(job, i)
+                    job["steps_done"] = i + 1
+
+            def band_step(job, i):
+                key_tiles = job["key_tiles"]
+                if i == 0:
+                    job["sums"] = [sum_psum.tile([P, BANK], F32, name="sum%d" % n) for n in range(E // BANK)]
+                if i < HEADS:
+                    bandT_ps = bandT_psum.tile([P, 2, P], F32, name="bandT_ps")
+                    for kt in key_tiles:
+                        nc.tensor.transpose(bandT_ps[:, kt, :], job["bands"][i // SET][kt][:, i % SET, :], ident[:])
+                    bandT = bandT_pool.tile([P, 2, P], F32, name="bandT")
+                    nc.scalar.copy(out=bandT[:, key_tiles[0] : 2, :], in_=bandT_ps[:, key_tiles[0] : 2, :])
+                    job["bandT"][i] = bandT
+                h = i - LAG
+                if h >= 0:
+                    for kt in key_tiles:
+                        nc.tensor.matmul(
+                            out=sum_cols(job, h),
+                            lhsT=job["bandT"][h][:, kt, :],
+                            rhs=job["v_near"][kt][:, h * HEAD_DIM : (h + 1) * HEAD_DIM],
+                            start=(kt == key_tiles[0]),
+                            stop=(kt == key_tiles[-1]),
+                        )
+
+            def add_up(score, partial, run):
+                nc.vector.tensor_reduce(
+                    out=score[:, run[0] : run[0] + len(run), :],
+                    in_=partial[:, 0 : len(run), :].rearrange("p s (h b) -> p s h b", b=GROUPS),
+                    axis=AXIS.X,
+                    op=ALU.add,
+                )
+
+            def scores(t, job):
                 score = lag_pool.tile([P, SLOTS, HEADS], F32, name="score")
                 live = [s for s in range(SLOTS) if OFFSETS[s] < (t + 1) * P]
                 if len(live) < SLOTS:
                     nc.vector.memset(score[:], 0.0)
+                done = 0
+                unread = None
                 for run in runs_of_slots(live, BLOCKS):
                     partial = score_psum.tile([P, BLOCKS, P], F32, name="partial")
                     for i, s in enumerate(run):
@@ -247,6 +291,9 @@ def tile_dwarfattention_pa_kernel(tc, x, W_qkv, b_qkv, gains, pos_bias, identity
                             in1=k_feat[:, :, first : first + P],
                             op=ALU.mult,
                         )
+                        if unread is not None and i == min(1, len(run) - 1):
+                            add_up(score, *unread)
+                            unread = None
                         for a in range(GROUPS):
                             nc.tensor.matmul(
                                 out=partial[:, i, :],
@@ -256,15 +303,13 @@ def tile_dwarfattention_pa_kernel(tc, x, W_qkv, b_qkv, gains, pos_bias, identity
                                 start=(a == 0),
                                 stop=(a == GROUPS - 1),
                             )
-                    nc.vector.tensor_reduce(
-                        out=score[:, run[0] : run[0] + len(run), :],
-                        in_=partial[:, 0 : len(run), :].rearrange("p s (h b) -> p s h b", b=GROUPS),
-                        axis=AXIS.X,
-                        op=ALU.add,
-                    )
-                return score
+                        done += 1
+                        if job is not None and done > BAND_START:
+                            band_steps(job, BAND_PACE)
+                    unread = (partial, run)
+                return score, unread
 
-            def weights(t, score, tap_gain):
+            def tap_features(t, score, tap_gain):
                 g_jh = gains_sb[:, :, t, :].rearrange("p h j -> p j h")
                 nc.scalar.mul(out=tap_gain[:, 0:11, :], in_=g_jh, mul=D4[0])
                 nc.scalar.mul(out=tap_gain[:, TAU1 : TAU1 + 11, :], in_=g_jh, mul=D4[1])
@@ -294,11 +339,23 @@ def tile_dwarfattention_pa_kernel(tc, x, W_qkv, b_qkv, gains, pos_bias, identity
                     op=ALU.add,
                 )
                 feat = mid_pool.tile([P, ENTRIES, HEADS], F32, name="feat")
+                nc.scalar.activation(
+                    out=feat[:].rearrange("p e h -> p (e h)"),
+                    in_=u_plus_1[:].rearrange("p e h -> p (e h)"),
+                    func=ACT.Exp,
+                    bias=-1.0,
+                )
+                return u_plus_1, feat
+
+            def tap_weights(u_plus_1, feat, tap_gain):
                 feat_flat = feat[:].rearrange("p e h -> p (e h)")
-                u_flat = u_plus_1[:].rearrange("p e h -> p (e h)")
-                nc.scalar.activation(out=feat_flat, in_=u_flat, func=ACT.Exp, bias=-1.0)
                 nc.vector.scalar_tensor_tensor(
-                    out=feat_flat, in0=feat_flat, scalar=1.0, in1=u_flat, op0=ALU.min, op1=ALU.max
+                    out=feat_flat,
+                    in0=feat_flat,
+                    scalar=1.0,
+                    in1=u_plus_1[:].rearrange("p e h -> p (e h)"),
+                    op0=ALU.min,
+                    op1=ALU.max,
                 )
                 tap_mass = mid_pool.tile([P, TAU3, HEADS], F32, name="tap_mass")
                 mass = mid_pool.tile([P, SLOTS, HEADS], F32, name="mass")
@@ -374,42 +431,19 @@ def tile_dwarfattention_pa_kernel(tc, x, W_qkv, b_qkv, gains, pos_bias, identity
                     tiles.append((s, v_far))
                 return tiles
 
-            def weighted_sums(t, weight, bands, v_near, v_far):
-                key_tiles = [0, 1] if t > 0 else [1]
-                sums = [sum_psum.tile([P, BANK], F32, name="sum%d" % i) for i in range(E // BANK)]
-                for hs in range(HEAD_SETS):
-                    bandT = {}
-                    for kt in key_tiles:
-                        bandT_ps = bandT_psum.tile([P, SET, P], F32, name="bandT_ps")
-                        for i in range(SET):
-                            nc.tensor.transpose(bandT_ps[:, i, :], bands[hs][kt][:, i, :], ident[:])
-                        bandT[kt] = bandT_pool.tile([P, SET, P], F32, name="bandT")
-                        nc.scalar.copy(out=bandT[kt][:], in_=bandT_ps[:])
-                    for i in range(SET):
-                        h = hs * SET + i
-                        for kt in key_tiles:
-                            nc.tensor.matmul(
-                                out=sums[h * HEAD_DIM // BANK][:, h * HEAD_DIM % BANK : h * HEAD_DIM % BANK + HEAD_DIM],
-                                lhsT=bandT[kt][:, i, :],
-                                rhs=v_near[t - 1 + kt][:, h * HEAD_DIM : (h + 1) * HEAD_DIM],
-                                start=(kt == key_tiles[0]),
-                                stop=(kt == key_tiles[-1]),
-                            )
+            def far_sums(job):
                 result = lag_pool.tile([P, E], F32, name="result")
-                if not v_far:
-                    for i in range(E // BANK):
-                        nc.vector.tensor_copy(out=result[:, i * BANK : (i + 1) * BANK], in_=sums[i][:])
-                for count, (s, v_o) in enumerate(v_far):
+                if not job["v_far"]:
+                    for n in range(E // BANK):
+                        nc.vector.tensor_copy(out=result[:, n * BANK : (n + 1) * BANK], in_=job["sums"][n][:])
+                for count, (s, v_o) in enumerate(job["v_far"]):
                     for h in range(HEADS):
                         cols = slice(h * HEAD_DIM, (h + 1) * HEAD_DIM)
-                        so_far = result[:, cols]
-                        if count == 0:
-                            so_far = sums[h * HEAD_DIM // BANK][:, h * HEAD_DIM % BANK : h * HEAD_DIM % BANK + HEAD_DIM]
                         nc.vector.scalar_tensor_tensor(
                             out=result[:, cols],
                             in0=v_o[:, cols],
-                            scalar=weight[:, s, h : h + 1],
-                            in1=so_far,
+                            scalar=job["weight"][:, s, h : h + 1],
+                            in1=sum_cols(job, h) if count == 0 else result[:, cols],
                             op0=ALU.mult,
                             op1=ALU.add,
                         )
@@ -418,17 +452,32 @@ def tile_dwarfattention_pa_kernel(tc, x, W_qkv, b_qkv, gains, pos_bias, identity
             def store(t, result):
                 nc.sync.dma_start(out=out_rows[t * P : (t + 1) * P, :], in_=result[:])
 
-            v_near = {TILES - 1: load_v_tile(TILES - 1)}
-            waiting = None
+            v_tiles = {TILES - 1: load_v_tile(TILES - 1)}
+            job = None
             for step, t in enumerate(reversed(range(TILES))):
-                weight = weights(t, scores(t), tap_gains[step % 2])
-                if waiting is not None:
-                    result = weighted_sums(*waiting)
-                bands = skew(t, weight)
-                if waiting is not None:
-                    store(t + 1, result)
+                tap_gain = tap_gains[step % 2]
+                score, unread = scores(t, job)
+                if job is not None:
+                    band_steps(job, HEADS + LAG)
+                add_up(score, *unread)
+                u_plus_1, feat = tap_features(t, score, tap_gain)
+                if job is not None:
+                    result = far_sums(job)
                 v_far = load_far(t)
                 if t > 0:
-                    v_near[t - 1] = load_v_tile(t - 1)
-                waiting = (t, weight, bands, v_near, v_far)
-            store(0, weighted_sums(*waiting))
+                    v_tiles[t - 1] = load_v_tile(t - 1)
+                weight = tap_weights(u_plus_1, feat, tap_gain)
+                bands = skew(t, weight)
+                if job is not None:
+                    store(t + 1, result)
+                job = {
+                    "steps_done": 0,
+                    "key_tiles": [0, 1] if t > 0 else [1],
+                    "weight": weight,
+                    "bands": bands,
+                    "bandT": {},
+                    "v_near": {0: v_tiles.get(t - 1), 1: v_tiles[t]},
+                    "v_far": v_far,
+                }
+            band_steps(job, HEADS + LAG)
+            store(0, far_sums(job))

@@ -47,8 +47,7 @@ HEAD_SETS = 4
 SET = HEADS // HEAD_SETS
 PITCH = 2 * P
 LAG = 2
-BAND_START = 8
-BAND_PACE = 2
+KEEP_ALIVE = 0
 
 FLOPS = 2 * TOKENS * D_IN * 3 * E + 4 * TOKENS * E * 42
 
@@ -112,6 +111,10 @@ def tile_dwarfattention_pa_kernel(tc, x, W_qkv, b_qkv, gains, pos_bias, identity
             nc.vector.tensor_tensor(out=tap_gain[:, LOCAL, :], in0=soft[:, 0, :], in1=soft[:, 2, :], op=ALU.add)
             tap_gains.append(tap_gain)
 
+        if KEEP_ALIVE:
+            idle_codes = const.tile([P, BANK], U32, name="idle_codes", align_bytes=64)
+            idle_scales = const.tile([P, BANK], U8, name="idle_scales", align_bytes=64)
+
         with ExitStack() as phase:
             raw_pool = phase.enter_context(tc.tile_pool(name="raw", bufs=3))
             grouped_pool = phase.enter_context(tc.tile_pool(name="grouped", bufs=2))
@@ -146,6 +149,11 @@ def tile_dwarfattention_pa_kernel(tc, x, W_qkv, b_qkv, gains, pos_bias, identity
                         nc.scalar.copy(out=dst, in_=src)
                 for g in range(PASSES):
                     nc.vector.quantize_mx(out=codes[:, g, :].bitcast(FP8X4), scales=scales[:, g, :], in_=grouped[:, g, :])
+
+            if KEEP_ALIVE:
+                ones = grouped_pool.tile([P, BANK * PACK], BF16, name="ones", bufs=1, align_bytes=64)
+                nc.vector.memset(ones[:], 1.0)
+                nc.vector.quantize_mx(out=idle_codes[:].bitcast(FP8X4), scales=idle_scales[:], in_=ones[:])
 
             x_codes = x_pool.tile([P, PASSES, TOKENS], U32, name="x_codes", align_bytes=64)
             x_scales = x_pool.tile([P, PASSES, TOKENS], U8, name="x_scales", align_bytes=64)
@@ -217,7 +225,7 @@ def tile_dwarfattention_pa_kernel(tc, x, W_qkv, b_qkv, gains, pos_bias, identity
         with ExitStack() as phase:
             prod_pool = phase.enter_context(tc.tile_pool(name="prod", bufs=4))
             mid_pool = phase.enter_context(tc.tile_pool(name="mid", bufs=1))
-            lag_pool = phase.enter_context(tc.tile_pool(name="lag", bufs=2))
+            lag_pool = phase.enter_context(tc.tile_pool(name="lag", bufs=3))
             band_pool = phase.enter_context(tc.tile_pool(name="band", bufs=2 * HEAD_SETS))
             bandT_pool = phase.enter_context(tc.tile_pool(name="bandT", bufs=4))
             near_pool = phase.enter_context(tc.tile_pool(name="v_near", bufs=2))
@@ -225,6 +233,8 @@ def tile_dwarfattention_pa_kernel(tc, x, W_qkv, b_qkv, gains, pos_bias, identity
             score_psum = phase.enter_context(tc.psum_pool(name="score", bufs=2))
             bandT_psum = phase.enter_context(tc.psum_pool(name="bandT_ps", bufs=2))
             sum_psum = phase.enter_context(tc.psum_pool(name="sum", bufs=1))
+            idle_psum = phase.enter_context(tc.psum_pool(name="idle", bufs=1))
+            phase.enter_context(tc.manual_schedule())
 
             band_rows = mid_pool.tile([P, HEADS, PITCH], F32, name="band_rows")
             nc.vector.memset(band_rows[:], 0.0)
@@ -238,15 +248,16 @@ def tile_dwarfattention_pa_kernel(tc, x, W_qkv, b_qkv, gains, pos_bias, identity
                 first = h * HEAD_DIM % BANK
                 return job["sums"][h * HEAD_DIM // BANK][:, first : first + HEAD_DIM]
 
-            def band_steps(job, count):
-                for i in range(job["steps_done"], min(job["steps_done"] + count, HEADS + LAG)):
+            def band_sums(job):
+                job["sums"] = [sum_psum.tile([P, BANK], F32, name="sum%d" % n) for n in range(E // BANK)]
+                for i in range(HEADS + LAG):
                     band_step(job, i)
-                    job["steps_done"] = i + 1
+                job["result"] = lag_pool.tile([P, E], F32, name="result")
+                for n in range(E // BANK):
+                    nc.scalar.copy(out=job["result"][:, n * BANK : (n + 1) * BANK], in_=job["sums"][n][:])
 
             def band_step(job, i):
                 key_tiles = job["key_tiles"]
-                if i == 0:
-                    job["sums"] = [sum_psum.tile([P, BANK], F32, name="sum%d" % n) for n in range(E // BANK)]
                 if i < HEADS:
                     bandT_ps = bandT_psum.tile([P, 2, P], F32, name="bandT_ps")
                     for kt in key_tiles:
@@ -273,8 +284,8 @@ def tile_dwarfattention_pa_kernel(tc, x, W_qkv, b_qkv, gains, pos_bias, identity
                     op=ALU.add,
                 )
 
-            def scores(t, job):
-                score = lag_pool.tile([P, SLOTS, HEADS], F32, name="score")
+            def scores(t):
+                score = lag_pool.tile([P, SLOTS, HEADS], F32, name="score", bufs=2)
                 live = [s for s in range(SLOTS) if OFFSETS[s] < (t + 1) * P]
                 if len(live) < SLOTS:
                     nc.vector.memset(score[:], 0.0)
@@ -304,8 +315,18 @@ def tile_dwarfattention_pa_kernel(tc, x, W_qkv, b_qkv, gains, pos_bias, identity
                                 stop=(a == GROUPS - 1),
                             )
                         done += 1
-                        if job is not None and done > BAND_START:
-                            band_steps(job, BAND_PACE)
+                        if done % 2 == 0:
+                            for n in range(KEEP_ALIVE):
+                                idle = idle_psum.tile([P, BANK], F32, name="idle")
+                                nc.tensor.matmul_mx(
+                                    out=idle[:],
+                                    lhsT=idle_codes[:, 0:P].bitcast(FP8X4),
+                                    lhsT_scale=idle_scales[:, 0:P],
+                                    rhs=idle_codes[:].bitcast(FP8X4),
+                                    rhs_scale=idle_scales[:],
+                                    start=True,
+                                    stop=True,
+                                )
                     unread = (partial, run)
                 return score, unread
 
@@ -431,53 +452,48 @@ def tile_dwarfattention_pa_kernel(tc, x, W_qkv, b_qkv, gains, pos_bias, identity
                     tiles.append((s, v_far))
                 return tiles
 
-            def far_sums(job):
-                result = lag_pool.tile([P, E], F32, name="result")
-                if not job["v_far"]:
-                    for n in range(E // BANK):
-                        nc.vector.tensor_copy(out=result[:, n * BANK : (n + 1) * BANK], in_=job["sums"][n][:])
-                for count, (s, v_o) in enumerate(job["v_far"]):
+            def far_sums(job, part):
+                result = job["result"]
+                for s, v_o in job["v_far"][part::2]:
                     for h in range(HEADS):
                         cols = slice(h * HEAD_DIM, (h + 1) * HEAD_DIM)
                         nc.vector.scalar_tensor_tensor(
                             out=result[:, cols],
                             in0=v_o[:, cols],
                             scalar=job["weight"][:, s, h : h + 1],
-                            in1=sum_cols(job, h) if count == 0 else result[:, cols],
+                            in1=result[:, cols],
                             op0=ALU.mult,
                             op1=ALU.add,
                         )
-                return result
-
-            def store(t, result):
-                nc.sync.dma_start(out=out_rows[t * P : (t + 1) * P, :], in_=result[:])
 
             v_tiles = {TILES - 1: load_v_tile(TILES - 1)}
-            job = None
-            for step, t in enumerate(reversed(range(TILES))):
-                tap_gain = tap_gains[step % 2]
-                score, unread = scores(t, job)
-                if job is not None:
-                    band_steps(job, HEADS + LAG)
-                add_up(score, *unread)
-                u_plus_1, feat = tap_features(t, score, tap_gain)
-                if job is not None:
-                    result = far_sums(job)
-                v_far = load_far(t)
+            jobs = {}
+            for step in range(TILES + 2):
+                t = TILES - 1 - step
+                band_job = jobs.get(t + 1)
+                far_job = jobs.get(t + 2)
+                if t >= 0:
+                    score, unread = scores(t)
+                if far_job is not None:
+                    far_sums(far_job, 0)
+                if t >= 0:
+                    add_up(score, *unread)
+                    u_plus_1, feat = tap_features(t, score, tap_gains[step % 2])
+                if band_job is not None:
+                    band_sums(band_job)
+                if far_job is not None:
+                    far_sums(far_job, 1)
+                    nc.sync.dma_start(out=out_rows[(t + 2) * P : (t + 3) * P, :], in_=far_job["result"][:])
+                if band_job is not None:
+                    band_job["v_far"] = load_far(t + 1)
                 if t > 0:
                     v_tiles[t - 1] = load_v_tile(t - 1)
-                weight = tap_weights(u_plus_1, feat, tap_gain)
-                bands = skew(t, weight)
-                if job is not None:
-                    store(t + 1, result)
-                job = {
-                    "steps_done": 0,
-                    "key_tiles": [0, 1] if t > 0 else [1],
-                    "weight": weight,
-                    "bands": bands,
-                    "bandT": {},
-                    "v_near": {0: v_tiles.get(t - 1), 1: v_tiles[t]},
-                    "v_far": v_far,
-                }
-            band_steps(job, HEADS + LAG)
-            store(0, far_sums(job))
+                if t >= 0:
+                    weight = tap_weights(u_plus_1, feat, tap_gains[step % 2])
+                    jobs[t] = {
+                        "key_tiles": [0, 1] if t > 0 else [1],
+                        "weight": weight,
+                        "bands": skew(t, weight),
+                        "bandT": {},
+                        "v_near": {0: v_tiles.get(t - 1), 1: v_tiles[t]},
+                    }

@@ -47,7 +47,7 @@ HEAD_SETS = 4
 SET = HEADS // HEAD_SETS
 PITCH = 2 * P
 LAG = 2
-KEEP_ALIVE = 0
+KEEP_ALIVE = 2
 
 FLOPS = 2 * TOKENS * D_IN * 3 * E + 4 * TOKENS * E * 42
 

@@ -47,7 +47,6 @@ HEAD_SETS = 4
 SET = HEADS // HEAD_SETS
 PITCH = 2 * P
 LAG = 2
-KEEP_ALIVE = 2
 
 FLOPS = 2 * TOKENS * D_IN * 3 * E + 4 * TOKENS * E * 42
 
@@ -74,7 +73,7 @@ def tile_dwarfattention_pa_kernel(tc, x, W_qkv, b_qkv, gains, pos_bias, identity
         ident = const.tile([P, P], F32, name="ident")
         make_identity(nc, ident[:])
 
-        q_feat = keep.tile([P, GROUPS, TOKENS], F32, name="q_feat")
+        q_tok = keep.tile([P, TILES, E], F32, name="q_tok")
         k_feat = keep.tile([P, GROUPS, PAD + TOKENS], F32, name="k_feat")
         nc.vector.memset(k_feat[:, :, 0:PAD], 0.0)
 
@@ -111,10 +110,6 @@ def tile_dwarfattention_pa_kernel(tc, x, W_qkv, b_qkv, gains, pos_bias, identity
             nc.vector.tensor_tensor(out=tap_gain[:, LOCAL, :], in0=soft[:, 0, :], in1=soft[:, 2, :], op=ALU.add)
             tap_gains.append(tap_gain)
 
-        if KEEP_ALIVE:
-            idle_codes = const.tile([P, BANK], U32, name="idle_codes", align_bytes=64)
-            idle_scales = const.tile([P, BANK], U8, name="idle_scales", align_bytes=64)
-
         with ExitStack() as phase:
             raw_pool = phase.enter_context(tc.tile_pool(name="raw", bufs=3))
             grouped_pool = phase.enter_context(tc.tile_pool(name="grouped", bufs=2))
@@ -150,11 +145,6 @@ def tile_dwarfattention_pa_kernel(tc, x, W_qkv, b_qkv, gains, pos_bias, identity
                 for g in range(PASSES):
                     nc.vector.quantize_mx(out=codes[:, g, :].bitcast(FP8X4), scales=scales[:, g, :], in_=grouped[:, g, :])
 
-            if KEEP_ALIVE:
-                ones = grouped_pool.tile([P, BANK * PACK], BF16, name="ones", bufs=1, align_bytes=64)
-                nc.vector.memset(ones[:], 1.0)
-                nc.vector.quantize_mx(out=idle_codes[:].bitcast(FP8X4), scales=idle_scales[:], in_=ones[:])
-
             x_codes = x_pool.tile([P, PASSES, TOKENS], U32, name="x_codes", align_bytes=64)
             x_scales = x_pool.tile([P, PASSES, TOKENS], U8, name="x_scales", align_bytes=64)
             x_blocks = x.rearrange("o (n c p) k -> (o n) p c k", c=BLOCKS, p=P)
@@ -171,41 +161,34 @@ def tile_dwarfattention_pa_kernel(tc, x, W_qkv, b_qkv, gains, pos_bias, identity
                 return w_codes, w_scales
 
             w_by_group = W_qkv.rearrange("(s r a) k -> s r a k", s=3, a=GROUPS)
-            for third, dest, pad in ((0, q_feat, 0), (1, k_feat, PAD)):
-                w_codes, w_scales = quantise_third(
-                    [w_by_group[third][:, n * BLOCKS : (n + 1) * BLOCKS, :] for n in range(E // BANK)]
-                )
-                for a in range(GROUPS):
-                    feats = slice(a * P, (a + 1) * P)
-                    for n in range(TOKENS // BANK):
-                        toks = slice(n * BANK, (n + 1) * BANK)
-                        acc = acc_psum.tile([P, BANK], F32, name="acc")
-                        for g in range(PASSES):
-                            nc.tensor.matmul_mx(
-                                out=acc[:],
-                                lhsT=w_codes[:, g, feats].bitcast(FP8X4),
-                                lhsT_scale=w_scales[:, g, feats],
-                                rhs=x_codes[:, g, toks].bitcast(FP8X4),
-                                rhs_scale=x_scales[:, g, toks],
-                                start=(g == 0),
-                                stop=(g == PASSES - 1),
-                            )
-                        dst = dest[:, a, pad + n * BANK : pad + (n + 1) * BANK]
-                        bias = bias_qk[:, third, a : a + 1]
-                        if n % 2 == 0:
-                            nc.scalar.activation(out=dst, in_=acc[:], func=ACT.Identity, bias=bias)
-                        else:
-                            nc.vector.tensor_scalar_add(out=dst, in0=acc[:], scalar1=bias)
 
-            w_natural = W_qkv.rearrange("(s n c p) k -> s n p c k", s=3, c=BLOCKS, p=P)
-            w_codes, w_scales = quantise_third([w_natural[2][n] for n in range(E // BANK)])
-            nc.sync.dma_start(
-                out=gains_sb[:].rearrange("p h t j -> p (h t) j"),
-                in_=gains.rearrange("o h (t p) j -> p (o h t) j", p=P),
+            w_codes, w_scales = quantise_third(
+                [w_by_group[1][:, n * BLOCKS : (n + 1) * BLOCKS, :] for n in range(E // BANK)]
             )
-            for t in range(TILES):
+            for a in range(GROUPS):
+                feats = slice(a * P, (a + 1) * P)
+                for n in range(TOKENS // BANK):
+                    toks = slice(n * BANK, (n + 1) * BANK)
+                    acc = acc_psum.tile([P, BANK], F32, name="acc")
+                    for g in range(PASSES):
+                        nc.tensor.matmul_mx(
+                            out=acc[:],
+                            lhsT=w_codes[:, g, feats].bitcast(FP8X4),
+                            lhsT_scale=w_scales[:, g, feats],
+                            rhs=x_codes[:, g, toks].bitcast(FP8X4),
+                            rhs_scale=x_scales[:, g, toks],
+                            start=(g == 0),
+                            stop=(g == PASSES - 1),
+                        )
+                    dst = k_feat[:, a, PAD + n * BANK : PAD + (n + 1) * BANK]
+                    bias = bias_qk[:, 1, a : a + 1]
+                    if n % 2 == 0:
+                        nc.scalar.activation(out=dst, in_=acc[:], func=ACT.Identity, bias=bias)
+                    else:
+                        nc.vector.tensor_scalar_add(out=dst, in0=acc[:], scalar1=bias)
+
+            def project_tokens(t, w_codes, w_scales, bias_all, dest):
                 toks = slice(t * P, (t + 1) * P)
-                v_stage = v_pool.tile([P, E], F32, name="v_stage")
                 for n in range(E // BANK):
                     feats = slice(n * BANK, (n + 1) * BANK)
                     acc = acc_psum.tile([P, BANK], F32, name="acc")
@@ -219,13 +202,42 @@ def tile_dwarfattention_pa_kernel(tc, x, W_qkv, b_qkv, gains, pos_bias, identity
                             start=(g == 0),
                             stop=(g == PASSES - 1),
                         )
-                    nc.vector.tensor_tensor(out=v_stage[:, feats], in0=acc[:], in1=bias_v[:, feats], op=ALU.add)
-                nc.sync.dma_start(out=out_rows[toks, :], in_=v_stage[:])
+                    nc.vector.tensor_tensor(out=dest[:, feats], in0=acc[:], in1=bias_all[:, feats], op=ALU.add)
+
+            bias_q = v_pool.tile([P, E], F32, name="bias_q", bufs=1)
+            for n in range(E // BANK):
+                acc = acc_psum.tile([P, BANK], F32, name="acc")
+                for c in range(BLOCKS):
+                    a = n * BLOCKS + c
+                    nc.tensor.matmul(
+                        out=acc[:, c * P : (c + 1) * P],
+                        lhsT=bias_qk[:, 0, a : a + 1].to_broadcast([P, P]),
+                        rhs=ident[:],
+                        start=True,
+                        stop=True,
+                    )
+                nc.scalar.copy(out=bias_q[:, n * BANK : (n + 1) * BANK], in_=acc[:])
+            w_codes, w_scales = quantise_third(
+                [w_by_group[0][:, n * BLOCKS : (n + 1) * BLOCKS, :] for n in range(E // BANK)]
+            )
+            for t in range(TILES):
+                project_tokens(t, w_codes, w_scales, bias_q, q_tok[:, t, :])
+
+            w_natural = W_qkv.rearrange("(s n c p) k -> s n p c k", s=3, c=BLOCKS, p=P)
+            w_codes, w_scales = quantise_third([w_natural[2][n] for n in range(E // BANK)])
+            nc.sync.dma_start(
+                out=gains_sb[:].rearrange("p h t j -> p (h t) j"),
+                in_=gains.rearrange("o h (t p) j -> p (o h t) j", p=P),
+            )
+            for t in range(TILES):
+                v_stage = v_pool.tile([P, E], F32, name="v_stage")
+                project_tokens(t, w_codes, w_scales, bias_v, v_stage)
+                nc.sync.dma_start(out=out_rows[t * P : (t + 1) * P, :], in_=v_stage[:])
 
         with ExitStack() as phase:
-            prod_pool = phase.enter_context(tc.tile_pool(name="prod", bufs=4))
+            prod_pool = phase.enter_context(tc.tile_pool(name="prod", bufs=6))
             mid_pool = phase.enter_context(tc.tile_pool(name="mid", bufs=1))
-            lag_pool = phase.enter_context(tc.tile_pool(name="lag", bufs=3))
+            lag_pool = phase.enter_context(tc.tile_pool(name="lag", bufs=2))
             band_pool = phase.enter_context(tc.tile_pool(name="band", bufs=2 * HEAD_SETS))
             bandT_pool = phase.enter_context(tc.tile_pool(name="bandT", bufs=4))
             near_pool = phase.enter_context(tc.tile_pool(name="v_near", bufs=2))
@@ -233,7 +245,7 @@ def tile_dwarfattention_pa_kernel(tc, x, W_qkv, b_qkv, gains, pos_bias, identity
             score_psum = phase.enter_context(tc.psum_pool(name="score", bufs=2))
             bandT_psum = phase.enter_context(tc.psum_pool(name="bandT_ps", bufs=2))
             sum_psum = phase.enter_context(tc.psum_pool(name="sum", bufs=1))
-            idle_psum = phase.enter_context(tc.psum_pool(name="idle", bufs=1))
+            q_psum = phase.enter_context(tc.psum_pool(name="q", bufs=1))
             phase.enter_context(tc.manual_schedule())
 
             band_rows = mid_pool.tile([P, HEADS, PITCH], F32, name="band_rows")
@@ -284,49 +296,50 @@ def tile_dwarfattention_pa_kernel(tc, x, W_qkv, b_qkv, gains, pos_bias, identity
                     op=ALU.add,
                 )
 
-            def scores(t):
-                score = lag_pool.tile([P, SLOTS, HEADS], F32, name="score", bufs=2)
+            def turn_and_add(partial, i, prod, groups):
+                for a in range(groups):
+                    nc.tensor.matmul(
+                        out=partial[:, i, :],
+                        lhsT=prod[:, a, :],
+                        rhs=ident[:],
+                        is_transpose=True,
+                        start=(a == 0),
+                        stop=(a == groups - 1),
+                    )
+
+            def turn_q(t):
+                q_feat = [q_psum.tile([P, BLOCKS, P], F32, name="q_feat%d" % n) for n in range(GROUPS // BLOCKS)]
+                for a in range(GROUPS):
+                    nc.tensor.transpose(q_feat[a // BLOCKS][:, a % BLOCKS, :], q_tok[:, t, a * P : (a + 1) * P], ident[:])
+                return q_feat
+
+            def scores(t, q_feat):
+                score = lag_pool.tile([P, SLOTS, HEADS], F32, name="score", bufs=1)
                 live = [s for s in range(SLOTS) if OFFSETS[s] < (t + 1) * P]
                 if len(live) < SLOTS:
                     nc.vector.memset(score[:], 0.0)
-                done = 0
+                half = GROUPS // 2
                 unread = None
                 for run in runs_of_slots(live, BLOCKS):
                     partial = score_psum.tile([P, BLOCKS, P], F32, name="partial")
                     for i, s in enumerate(run):
                         first = PAD + t * P - OFFSETS[s]
                         prod = prod_pool.tile([P, GROUPS, P], F32, name="prod")
-                        nc.vector.tensor_tensor(
-                            out=prod[:],
-                            in0=q_feat[:, :, t * P : (t + 1) * P],
-                            in1=k_feat[:, :, first : first + P],
-                            op=ALU.mult,
-                        )
-                        if unread is not None and i == min(1, len(run) - 1):
+                        for n in range(GROUPS // BLOCKS):
+                            groups = slice(n * BLOCKS, (n + 1) * BLOCKS)
+                            nc.vector.tensor_tensor(
+                                out=prod[:, groups, :], in0=q_feat[n][:], in1=k_feat[:, groups, first : first + P], op=ALU.mult
+                            )
+                        if unread is not None and i == len(run) - 1:
                             add_up(score, *unread)
                             unread = None
-                        for a in range(GROUPS):
-                            nc.tensor.matmul(
-                                out=partial[:, i, :],
-                                lhsT=prod[:, a, :],
-                                rhs=ident[:],
-                                is_transpose=True,
-                                start=(a == 0),
-                                stop=(a == GROUPS - 1),
+                        if i % 2 == 1:
+                            nc.gpsimd.tensor_tensor(
+                                out=prod[:, 0:half, :], in0=prod[:, 0:half, :], in1=prod[:, half:GROUPS, :], op=ALU.add
                             )
-                        done += 1
-                        if done % 2 == 0:
-                            for n in range(KEEP_ALIVE):
-                                idle = idle_psum.tile([P, BANK], F32, name="idle")
-                                nc.tensor.matmul_mx(
-                                    out=idle[:],
-                                    lhsT=idle_codes[:, 0:P].bitcast(FP8X4),
-                                    lhsT_scale=idle_scales[:, 0:P],
-                                    rhs=idle_codes[:].bitcast(FP8X4),
-                                    rhs_scale=idle_scales[:],
-                                    start=True,
-                                    stop=True,
-                                )
+                            turn_and_add(partial, i, prod, half)
+                        else:
+                            turn_and_add(partial, i, prod, GROUPS)
                     unread = (partial, run)
                 return score, unread
 
@@ -467,13 +480,16 @@ def tile_dwarfattention_pa_kernel(tc, x, W_qkv, b_qkv, gains, pos_bias, identity
                         )
 
             v_tiles = {TILES - 1: load_v_tile(TILES - 1)}
+            q_feat = turn_q(TILES - 1)
             jobs = {}
             for step in range(TILES + 2):
                 t = TILES - 1 - step
                 band_job = jobs.get(t + 1)
                 far_job = jobs.get(t + 2)
                 if t >= 0:
-                    score, unread = scores(t)
+                    score, unread = scores(t, q_feat)
+                if t > 0:
+                    q_feat = turn_q(t - 1)
                 if far_job is not None:
                     far_sums(far_job, 0)
                 if t >= 0:

@@ -311,35 +311,42 @@ def tile_dwarfattention_pa_kernel(tc, x, W_qkv, b_qkv, gains, pos_bias, identity
                 q_feat = [q_psum.tile([P, BLOCKS, P], F32, name="q_feat%d" % n) for n in range(GROUPS // BLOCKS)]
                 for a in range(GROUPS):
                     nc.tensor.transpose(q_feat[a // BLOCKS][:, a % BLOCKS, :], q_tok[:, t, a * P : (a + 1) * P], ident[:])
-                return q_feat
+                q_sb = mid_pool.tile([P, GROUPS, P], F32, name="q_sb")
+                for n in range(GROUPS // BLOCKS):
+                    nc.scalar.copy(out=q_sb[:, n * BLOCKS : (n + 1) * BLOCKS, :], in_=q_feat[n][:])
+                return q_feat, q_sb
 
-            def scores(t, q_feat):
+            def scores(t, q_pair):
                 score = lag_pool.tile([P, SLOTS, HEADS], F32, name="score", bufs=1)
                 live = [s for s in range(SLOTS) if OFFSETS[s] < (t + 1) * P]
                 if len(live) < SLOTS:
                     nc.vector.memset(score[:], 0.0)
-                half = GROUPS // 2
+                q_feat, q_sb = q_pair
                 unread = None
+                unit = 0
                 for run in runs_of_slots(live, BLOCKS):
                     partial = score_psum.tile([P, BLOCKS, P], F32, name="partial")
                     for i, s in enumerate(run):
                         first = PAD + t * P - OFFSETS[s]
                         prod = prod_pool.tile([P, GROUPS, P], F32, name="prod")
-                        for n in range(GROUPS // BLOCKS):
-                            groups = slice(n * BLOCKS, (n + 1) * BLOCKS)
-                            nc.vector.tensor_tensor(
-                                out=prod[:, groups, :], in0=q_feat[n][:], in1=k_feat[:, groups, first : first + P], op=ALU.mult
+                        if unit % 3 == 1:
+                            nc.gpsimd.tensor_tensor(
+                                out=prod[:], in0=q_sb[:], in1=k_feat[:, :, first : first + P], op=ALU.mult
                             )
+                        else:
+                            for n in range(GROUPS // BLOCKS):
+                                groups = slice(n * BLOCKS, (n + 1) * BLOCKS)
+                                nc.vector.tensor_tensor(
+                                    out=prod[:, groups, :],
+                                    in0=q_feat[n][:],
+                                    in1=k_feat[:, groups, first : first + P],
+                                    op=ALU.mult,
+                                )
+                        unit += 1
                         if unread is not None and i == len(run) - 1:
                             add_up(score, *unread)
                             unread = None
-                        if i % 2 == 1:
-                            nc.gpsimd.tensor_tensor(
-                                out=prod[:, 0:half, :], in0=prod[:, 0:half, :], in1=prod[:, half:GROUPS, :], op=ALU.add
-                            )
-                            turn_and_add(partial, i, prod, half)
-                        else:
-                            turn_and_add(partial, i, prod, GROUPS)
+                        turn_and_add(partial, i, prod, GROUPS)
                     unread = (partial, run)
                 return score, unread
 

@@ -46,6 +46,7 @@ ENTRIES = 43
 HEAD_SETS = 4
 SET = HEADS // HEAD_SETS
 PITCH = 2 * P
+GPSIMD_COLUMNS = 2
 LAG = 2
 
 FLOPS = 2 * TOKENS * D_IN * 3 * E + 4 * TOKENS * E * 42
@@ -432,8 +433,10 @@ def tile_dwarfattention_pa_kernel(tc, x, W_qkv, b_qkv, gains, pos_bias, identity
                 return weight
 
             def skew(t, weight):
-                for s in NEAR_SLOTS:
+                for s in NEAR_SLOTS[:-GPSIMD_COLUMNS]:
                     nc.scalar.copy(out=band_rows[:, :, BAND - OFFSETS[s]], in_=weight[:, s, :])
+                for s in NEAR_SLOTS[-GPSIMD_COLUMNS:]:
+                    nc.gpsimd.tensor_copy(out=band_rows[:, :, BAND - OFFSETS[s]], in_=weight[:, s, :])
                 free_tiles = [t, t + 1] if t + 1 < TILES else [t]
                 key_tiles = [0, 1] if t > 0 else [1]
                 bands = []

@@ -46,6 +46,7 @@ ENTRIES = 43
 HEAD_SETS = 4
 SET = HEADS // HEAD_SETS
 PITCH = 2 * P
+RAW_AHEAD = 5
 GPSIMD_COLUMNS = 2
 LAG = 2
 
@@ -112,22 +113,48 @@ def tile_dwarfattention_pa_kernel(tc, x, W_qkv, b_qkv, gains, pos_bias, identity
             tap_gains.append(tap_gain)
 
         with ExitStack() as phase:
-            raw_pool = phase.enter_context(tc.tile_pool(name="raw", bufs=3))
+            raw_pool = phase.enter_context(tc.tile_pool(name="raw", bufs=RAW_AHEAD))
             grouped_pool = phase.enter_context(tc.tile_pool(name="grouped", bufs=2))
             x_pool = phase.enter_context(tc.tile_pool(name="x_mx", bufs=1))
             w_pool = phase.enter_context(tc.tile_pool(name="w_mx", bufs=2))
             v_pool = phase.enter_context(tc.tile_pool(name="v_stage", bufs=3))
             turned_psum = phase.enter_context(tc.psum_pool(name="turned", bufs=4))
             acc_psum = phase.enter_context(tc.psum_pool(name="acc", bufs=4))
+            phase.enter_context(tc.manual_schedule())
 
             bias_v_bf = v_pool.tile([P, E], BF16, name="bias_v_bf", bufs=1)
             nc.scalar.dma_start(out=bias_v_bf[:], in_=b_qkv[2 * E : 3 * E].partition_broadcast(P))
             bias_v = v_pool.tile([P, E], F32, name="bias_v", bufs=1)
-            nc.vector.tensor_copy(out=bias_v[:], in_=bias_v_bf[:])
+            bias_q = v_pool.tile([P, E], F32, name="bias_q", bufs=1)
 
-            def quantise_512_rows(rows, codes, scales):
-                raw = raw_pool.tile([P, BLOCKS, D_IN], BF16, name="raw")
-                nc.sync.dma_start(out=raw[:], in_=rows)
+            x_blocks = x.rearrange("o (n c p) k -> (o n) p c k", c=BLOCKS, p=P)
+            w_by_group = W_qkv.rearrange("(s r a) k -> s r a k", s=3, a=GROUPS)
+            w_natural = W_qkv.rearrange("(s n c p) k -> s n p c k", s=3, c=BLOCKS, p=P)
+            rows_of = {}
+            for n in range(TOKENS // BANK):
+                rows_of["x%d" % n] = x_blocks[n]
+            for n in range(E // BANK):
+                rows_of["k%d" % n] = w_by_group[1][:, n * BLOCKS : (n + 1) * BLOCKS, :]
+                rows_of["q%d" % n] = w_by_group[0][:, n * BLOCKS : (n + 1) * BLOCKS, :]
+                rows_of["v%d" % n] = w_natural[2][n]
+            load_order = ["x0", "k0", "x1", "k1", "x2", "q0", "q1", "v0", "v1"]
+            raws = {}
+            groupeds = {}
+            mx = {}
+
+            x_codes = x_pool.tile([P, PASSES, TOKENS], U32, name="x_codes", align_bytes=64)
+            x_scales = x_pool.tile([P, PASSES, TOKENS], U8, name="x_scales", align_bytes=64)
+            mx["x"] = (x_codes, x_scales)
+
+            def load_next():
+                if len(raws) < len(load_order):
+                    piece = load_order[len(raws)]
+                    raw = raw_pool.tile([P, BLOCKS, D_IN], BF16, name="raw")
+                    nc.sync.dma_start(out=raw[:], in_=rows_of[piece])
+                    raws[piece] = raw
+
+            def turn(piece):
+                raw = raws[piece]
                 grouped = grouped_pool.tile([P, PASSES, BANK * PACK], BF16, name="grouped", align_bytes=64)
                 grouped_words = grouped[:].bitcast(F32).rearrange("p g (c u) -> p g c u", u=2)
                 for c in range(BLOCKS):
@@ -139,100 +166,114 @@ def tile_dwarfattention_pa_kernel(tc, x, W_qkv, b_qkv, gains, pos_bias, identity
                             nc.tensor.transpose(turned[:, g, u, :], raw_words[:, first : first + P], ident[:])
                     dst = grouped_words[:, :, c * P : (c + 1) * P, :]
                     src = turned[:].rearrange("p g u c -> p g c u")
-                    if c % 2 == 0:
+                    if c == 1:
                         nc.vector.tensor_copy(out=dst, in_=src)
                     else:
                         nc.scalar.copy(out=dst, in_=src)
-                for g in range(PASSES):
-                    nc.vector.quantize_mx(out=codes[:, g, :].bitcast(FP8X4), scales=scales[:, g, :], in_=grouped[:, g, :])
+                groupeds[piece] = grouped
+                load_next()
 
-            x_codes = x_pool.tile([P, PASSES, TOKENS], U32, name="x_codes", align_bytes=64)
-            x_scales = x_pool.tile([P, PASSES, TOKENS], U8, name="x_scales", align_bytes=64)
-            x_blocks = x.rearrange("o (n c p) k -> (o n) p c k", c=BLOCKS, p=P)
-            for n in range(TOKENS // BANK):
+            def quantise(piece):
+                kind, n = piece[0], int(piece[1])
+                if kind not in mx:
+                    w_codes = w_pool.tile([P, PASSES, E], U32, name="w_codes", align_bytes=64)
+                    w_scales = w_pool.tile([P, PASSES, E], U8, name="w_scales", align_bytes=64)
+                    mx[kind] = (w_codes, w_scales)
+                codes, scales = mx[kind]
                 cols = slice(n * BANK, (n + 1) * BANK)
-                quantise_512_rows(x_blocks[n], x_codes[:, :, cols], x_scales[:, :, cols])
+                for g in range(PASSES):
+                    nc.vector.quantize_mx(
+                        out=codes[:, g, cols].bitcast(FP8X4), scales=scales[:, g, cols], in_=groupeds[piece][:, g, :]
+                    )
 
-            def quantise_third(row_views):
-                w_codes = w_pool.tile([P, PASSES, E], U32, name="w_codes", align_bytes=64)
-                w_scales = w_pool.tile([P, PASSES, E], U8, name="w_scales", align_bytes=64)
-                for n, rows in enumerate(row_views):
-                    cols = slice(n * BANK, (n + 1) * BANK)
-                    quantise_512_rows(rows, w_codes[:, :, cols], w_scales[:, :, cols])
-                return w_codes, w_scales
+            def product(lhs, lhs_cols, rhs, rhs_cols):
+                acc = acc_psum.tile([P, BANK], F32, name="acc")
+                for g in range(PASSES):
+                    nc.tensor.matmul_mx(
+                        out=acc[:],
+                        lhsT=mx[lhs][0][:, g, lhs_cols].bitcast(FP8X4),
+                        lhsT_scale=mx[lhs][1][:, g, lhs_cols],
+                        rhs=mx[rhs][0][:, g, rhs_cols].bitcast(FP8X4),
+                        rhs_scale=mx[rhs][1][:, g, rhs_cols],
+                        start=(g == 0),
+                        stop=(g == PASSES - 1),
+                    )
+                return acc
 
-            w_by_group = W_qkv.rearrange("(s r a) k -> s r a k", s=3, a=GROUPS)
-
-            w_codes, w_scales = quantise_third(
-                [w_by_group[1][:, n * BLOCKS : (n + 1) * BLOCKS, :] for n in range(E // BANK)]
-            )
-            for a in range(GROUPS):
-                feats = slice(a * P, (a + 1) * P)
-                for n in range(TOKENS // BANK):
-                    toks = slice(n * BANK, (n + 1) * BANK)
-                    acc = acc_psum.tile([P, BANK], F32, name="acc")
-                    for g in range(PASSES):
-                        nc.tensor.matmul_mx(
-                            out=acc[:],
-                            lhsT=w_codes[:, g, feats].bitcast(FP8X4),
-                            lhsT_scale=w_scales[:, g, feats],
-                            rhs=x_codes[:, g, toks].bitcast(FP8X4),
-                            rhs_scale=x_scales[:, g, toks],
-                            start=(g == 0),
-                            stop=(g == PASSES - 1),
-                        )
+            def project_k(groups, n):
+                for a in groups:
+                    acc = product("k", slice(a * P, (a + 1) * P), "x", slice(n * BANK, (n + 1) * BANK))
                     dst = k_feat[:, a, PAD + n * BANK : PAD + (n + 1) * BANK]
                     bias = bias_qk[:, 1, a : a + 1]
-                    if n % 2 == 0:
+                    if a % 2 == 0:
                         nc.scalar.activation(out=dst, in_=acc[:], func=ACT.Identity, bias=bias)
                     else:
                         nc.vector.tensor_scalar_add(out=dst, in0=acc[:], scalar1=bias)
 
-            def project_tokens(t, w_codes, w_scales, bias_all, dest):
-                toks = slice(t * P, (t + 1) * P)
+            def project_tokens(t, kind, bias_all, dest):
                 for n in range(E // BANK):
                     feats = slice(n * BANK, (n + 1) * BANK)
-                    acc = acc_psum.tile([P, BANK], F32, name="acc")
-                    for g in range(PASSES):
-                        nc.tensor.matmul_mx(
-                            out=acc[:],
-                            lhsT=x_codes[:, g, toks].bitcast(FP8X4),
-                            lhsT_scale=x_scales[:, g, toks],
-                            rhs=w_codes[:, g, feats].bitcast(FP8X4),
-                            rhs_scale=w_scales[:, g, feats],
-                            start=(g == 0),
-                            stop=(g == PASSES - 1),
-                        )
+                    acc = product("x", slice(t * P, (t + 1) * P), kind, feats)
                     nc.vector.tensor_tensor(out=dest[:, feats], in0=acc[:], in1=bias_all[:, feats], op=ALU.add)
 
-            bias_q = v_pool.tile([P, E], F32, name="bias_q", bufs=1)
-            for n in range(E // BANK):
-                acc = acc_psum.tile([P, BANK], F32, name="acc")
-                for c in range(BLOCKS):
-                    a = n * BLOCKS + c
-                    nc.tensor.matmul(
-                        out=acc[:, c * P : (c + 1) * P],
-                        lhsT=bias_qk[:, 0, a : a + 1].to_broadcast([P, P]),
-                        rhs=ident[:],
-                        start=True,
-                        stop=True,
-                    )
-                nc.scalar.copy(out=bias_q[:, n * BANK : (n + 1) * BANK], in_=acc[:])
-            w_codes, w_scales = quantise_third(
-                [w_by_group[0][:, n * BLOCKS : (n + 1) * BLOCKS, :] for n in range(E // BANK)]
-            )
-            for t in range(TILES):
-                project_tokens(t, w_codes, w_scales, bias_q, q_tok[:, t, :])
+            def project_q(tiles):
+                for t in tiles:
+                    project_tokens(t, "q", bias_q, q_tok[:, t, :])
 
-            w_natural = W_qkv.rearrange("(s n c p) k -> s n p c k", s=3, c=BLOCKS, p=P)
-            w_codes, w_scales = quantise_third([w_natural[2][n] for n in range(E // BANK)])
+            def spread_bias_q():
+                for n in range(E // BANK):
+                    acc = acc_psum.tile([P, BANK], F32, name="acc")
+                    for c in range(BLOCKS):
+                        a = n * BLOCKS + c
+                        nc.tensor.matmul(
+                            out=acc[:, c * P : (c + 1) * P],
+                            lhsT=bias_qk[:, 0, a : a + 1].to_broadcast([P, P]),
+                            rhs=ident[:],
+                            start=True,
+                            stop=True,
+                        )
+                    nc.scalar.copy(out=bias_q[:, n * BANK : (n + 1) * BANK], in_=acc[:])
+
+            lower, upper = range(0, BLOCKS), range(BLOCKS, GROUPS)
+            for i in range(RAW_AHEAD):
+                load_next()
+            turn("x0")
+            turn("k0")
+            quantise("x0")
+            turn("x1")
+            quantise("k0")
+            spread_bias_q()
+            turn("k1")
+            quantise("x1")
+            project_k(lower, 0)
+            turn("x2")
+            quantise("k1")
+            project_k(lower, 1)
+            turn("q0")
+            quantise("x2")
+            project_k(upper, 0)
+            project_k(upper, 1)
+            turn("q1")
+            quantise("q0")
+            project_k(lower, 2)
+            quantise("q1")
+            nc.vector.tensor_copy(out=bias_v[:], in_=bias_v_bf[:])
+            project_k(upper, 2)
             nc.sync.dma_start(
                 out=gains_sb[:].rearrange("p h t j -> p (h t) j"),
                 in_=gains.rearrange("o h (t p) j -> p (o h t) j", p=P),
             )
+            project_q(range(0, 3))
+            turn("v0")
+            project_q(range(3, 6))
+            quantise("v0")
+            turn("v1")
+            project_q(range(6, 9))
+            quantise("v1")
+            project_q(range(9, TILES))
             for t in range(TILES):
                 v_stage = v_pool.tile([P, E], F32, name="v_stage")
-                project_tokens(t, w_codes, w_scales, bias_v, v_stage)
+                project_tokens(t, "v", bias_v, v_stage)
                 nc.sync.dma_start(out=out_rows[t * P : (t + 1) * P, :], in_=v_stage[:])
 
         with ExitStack() as phase:

@@ -516,19 +516,18 @@ def tile_dwarfattention_pa_kernel(tc, x, W_qkv, b_qkv, gains, pos_bias, identity
                     tiles.append((s, v_far))
                 return tiles
 
+            def scale_far(job):
+                for s, v_o in job["v_far"]:
+                    for h in range(HEADS):
+                        cols = slice(h * HEAD_DIM, (h + 1) * HEAD_DIM)
+                        nc.scalar.activation(
+                            out=v_o[:, cols], in_=v_o[:, cols], func=ACT.Copy, scale=job["weight"][:, s, h : h + 1]
+                        )
+
             def far_sums(job, part):
                 result = job["result"]
                 for s, v_o in job["v_far"][part::2]:
-                    for h in range(HEADS):
-                        cols = slice(h * HEAD_DIM, (h + 1) * HEAD_DIM)
-                        nc.vector.scalar_tensor_tensor(
-                            out=result[:, cols],
-                            in0=v_o[:, cols],
-                            scalar=job["weight"][:, s, h : h + 1],
-                            in1=result[:, cols],
-                            op0=ALU.mult,
-                            op1=ALU.add,
-                        )
+                    nc.vector.tensor_tensor(out=result[:], in0=result[:], in1=v_o[:], op=ALU.add)
 
             v_tiles = {TILES - 1: load_v_tile(TILES - 1)}
             q_feat = turn_q(TILES - 1)
@@ -537,6 +536,8 @@ def tile_dwarfattention_pa_kernel(tc, x, W_qkv, b_qkv, gains, pos_bias, identity
                 t = TILES - 1 - step
                 band_job = jobs.get(t + 1)
                 far_job = jobs.get(t + 2)
+                if far_job is not None:
+                    scale_far(far_job)
                 if t >= 0:
                     score, unread = scores(t, q_feat)
                 if t > 0:

@@ -295,7 +295,7 @@ def tile_dwarfattention_pa_kernel(tc, x, W_qkv, b_qkv, gains, pos_bias, identity
 
             def load_v_tile(t):
                 v_near = near_pool.tile([P, E], F32, name="v_near")
-                nc.sync.dma_start(out=v_near[:], in_=out_rows[t * P : (t + 1) * P, :])
+                nc.scalar.dma_start(out=v_near[:], in_=out_rows[t * P : (t + 1) * P, :])
                 return v_near
 
             def sum_cols(job, h):
@@ -475,7 +475,7 @@ def tile_dwarfattention_pa_kernel(tc, x, W_qkv, b_qkv, gains, pos_bias, identity
 
             def skew(t, weight):
                 for s in NEAR_SLOTS[:-GPSIMD_COLUMNS]:
-                    nc.scalar.copy(out=band_rows[:, :, BAND - OFFSETS[s]], in_=weight[:, s, :])
+                    nc.vector.tensor_copy(out=band_rows[:, :, BAND - OFFSETS[s]], in_=weight[:, s, :])
                 for s in NEAR_SLOTS[-GPSIMD_COLUMNS:]:
                     nc.gpsimd.tensor_copy(out=band_rows[:, :, BAND - OFFSETS[s]], in_=weight[:, s, :])
                 free_tiles = [t, t + 1] if t + 1 < TILES else [t]
@@ -549,13 +549,13 @@ def tile_dwarfattention_pa_kernel(tc, x, W_qkv, b_qkv, gains, pos_bias, identity
                     u_plus_1, feat = tap_features(t, score, tap_gains[step % 2])
                 if band_job is not None:
                     band_sums(band_job)
+                if t > 0:
+                    v_tiles[t - 1] = load_v_tile(t - 1)
                 if far_job is not None:
                     far_sums(far_job, 1)
                     nc.sync.dma_start(out=out_rows[(t + 2) * P : (t + 3) * P, :], in_=far_job["result"][:])
                 if band_job is not None:
                     band_job["v_far"] = load_far(t + 1)
-                if t > 0:
-                    v_tiles[t - 1] = load_v_tile(t - 1)
                 if t >= 0:
                     weight = tap_weights(u_plus_1, feat, tap_gains[step % 2])
                     jobs[t] = {

@@ -47,6 +47,7 @@ HEAD_SETS = 4
 SET = HEADS // HEAD_SETS
 PITCH = 2 * P
 RAW_AHEAD = 5
+SCALE_PIECES = 6
 GPSIMD_COLUMNS = 2
 LAG = 2
 
@@ -302,10 +303,10 @@ def tile_dwarfattention_pa_kernel(tc, x, W_qkv, b_qkv, gains, pos_bias, identity
                 first = h * HEAD_DIM % BANK
                 return job["sums"][h * HEAD_DIM // BANK][:, first : first + HEAD_DIM]
 
-            def band_sums(job):
+            def band_open(job):
                 job["sums"] = [sum_psum.tile([P, BANK], F32, name="sum%d" % n) for n in range(E // BANK)]
-                for i in range(HEADS + LAG):
-                    band_step(job, i)
+
+            def band_close(job):
                 job["result"] = lag_pool.tile([P, E], F32, name="result")
                 for n in range(E // BANK):
                     nc.scalar.copy(out=job["result"][:, n * BANK : (n + 1) * BANK], in_=job["sums"][n][:])
@@ -325,7 +326,7 @@ def tile_dwarfattention_pa_kernel(tc, x, W_qkv, b_qkv, gains, pos_bias, identity
                         nc.tensor.matmul(
                             out=sum_cols(job, h),
                             lhsT=job["bandT"][h][:, kt, :],
-                            rhs=job["v_near"][kt][:, h * HEAD_DIM : (h + 1) * HEAD_DIM],
+                            rhs=v_tiles[job["tile"] - 1 + kt][:, h * HEAD_DIM : (h + 1) * HEAD_DIM],
                             start=(kt == key_tiles[0]),
                             stop=(kt == key_tiles[-1]),
                         )
@@ -358,7 +359,7 @@ def tile_dwarfattention_pa_kernel(tc, x, W_qkv, b_qkv, gains, pos_bias, identity
                     nc.scalar.copy(out=q_sb[:, n * BLOCKS : (n + 1) * BLOCKS, :], in_=q_feat[n][:])
                 return q_feat, q_sb
 
-            def scores(t, q_pair):
+            def scores(t, q_pair, weave):
                 score = lag_pool.tile([P, SLOTS, HEADS], F32, name="score", bufs=1)
                 live = [s for s in range(SLOTS) if OFFSETS[s] < (t + 1) * P]
                 if len(live) < SLOTS:
@@ -384,13 +385,14 @@ def tile_dwarfattention_pa_kernel(tc, x, W_qkv, b_qkv, gains, pos_bias, identity
                                     in1=k_feat[:, groups, first : first + P],
                                     op=ALU.mult,
                                 )
-                        unit += 1
                         if unread is not None and i == len(run) - 1:
                             add_up(score, *unread)
                             unread = None
                         turn_and_add(partial, i, prod, GROUPS)
+                        weave(unit)
+                        unit += 1
                     unread = (partial, run)
-                return score, unread
+                return score, unread, unit
 
             def tap_features(t, score, tap_gain):
                 g_jh = gains_sb[:, :, t, :].rearrange("p h j -> p j h")
@@ -479,28 +481,35 @@ def tile_dwarfattention_pa_kernel(tc, x, W_qkv, b_qkv, gains, pos_bias, identity
                 for s in NEAR_SLOTS[-GPSIMD_COLUMNS:]:
                     nc.gpsimd.tensor_copy(out=band_rows[:, :, BAND - OFFSETS[s]], in_=weight[:, s, :])
                 free_tiles = [t, t + 1] if t + 1 < TILES else [t]
-                key_tiles = [0, 1] if t > 0 else [1]
-                bands = []
-                for first in range(0, HEAD_SETS, len(free_tiles)):
-                    places = [(first + i, out_words[r * P * E : (r + 1) * P * E]) for i, r in enumerate(free_tiles)]
-                    for hs, words in places:
-                        nc.sync.dma_start(
-                            out=words.rearrange("(h n c) -> n h c", h=SET, c=PITCH),
-                            in_=band_rows[:, hs * SET : (hs + 1) * SET, :],
-                        )
-                    for hs, words in places:
-                        by_head = words.rearrange("(h w) -> h w", h=SET)
-                        band = {}
-                        for kt in key_tiles:
-                            band[kt] = band_pool.tile([P, SET, P], F32, name="band")
-                            nc.sync.dma_start(
-                                out=band[kt][:],
-                                in_=by_head[:, kt * P : kt * P + P * (PITCH - 1)].rearrange(
-                                    "h (n c) -> n h c", c=PITCH - 1
-                                )[:, :, 0:P],
-                            )
-                        bands.append(band)
-                return bands
+                trip = {"free_tiles": free_tiles, "key_tiles": [0, 1] if t > 0 else [1], "bands": []}
+                for hs in range(len(free_tiles)):
+                    skew_out(trip, hs)
+                return trip
+
+            def skew_words(trip, hs):
+                r = trip["free_tiles"][hs % len(trip["free_tiles"])]
+                return out_words[r * P * E : (r + 1) * P * E]
+
+            def skew_out(trip, hs):
+                nc.sync.dma_start(
+                    out=skew_words(trip, hs).rearrange("(h n c) -> n h c", h=SET, c=PITCH),
+                    in_=band_rows[:, hs * SET : (hs + 1) * SET, :],
+                )
+
+            def skew_back(trip, hs):
+                by_head = skew_words(trip, hs).rearrange("(h w) -> h w", h=SET)
+                band = {}
+                for kt in trip["key_tiles"]:
+                    band[kt] = band_pool.tile([P, SET, P], F32, name="band")
+                    nc.sync.dma_start(
+                        out=band[kt][:],
+                        in_=by_head[:, kt * P : kt * P + P * (PITCH - 1)].rearrange("h (n c) -> n h c", c=PITCH - 1)[
+                            :, :, 0:P
+                        ],
+                    )
+                trip["bands"].append(band)
+                if hs + len(trip["free_tiles"]) < HEAD_SETS:
+                    skew_out(trip, hs + len(trip["free_tiles"]))
 
             def load_far(t):
                 tiles = []
@@ -516,52 +525,69 @@ def tile_dwarfattention_pa_kernel(tc, x, W_qkv, b_qkv, gains, pos_bias, identity
                     tiles.append((s, v_far))
                 return tiles
 
-            def scale_far(job):
-                for s, v_o in job["v_far"]:
-                    for h in range(HEADS):
-                        cols = slice(h * HEAD_DIM, (h + 1) * HEAD_DIM)
-                        nc.scalar.activation(
-                            out=v_o[:, cols], in_=v_o[:, cols], func=ACT.Copy, scale=job["weight"][:, s, h : h + 1]
-                        )
+            def scale_far(job, count):
+                for s, v_o, h in job["to_scale"][:count]:
+                    cols = slice(h * HEAD_DIM, (h + 1) * HEAD_DIM)
+                    nc.scalar.activation(
+                        out=v_o[:, cols], in_=v_o[:, cols], func=ACT.Copy, scale=job["weight"][:, s, h : h + 1]
+                    )
+                job["to_scale"] = job["to_scale"][count:]
 
             def far_sums(job, part):
                 result = job["result"]
                 for s, v_o in job["v_far"][part::2]:
                     nc.vector.tensor_tensor(out=result[:], in0=result[:], in1=v_o[:], op=ALU.add)
 
-            v_tiles = {TILES - 1: load_v_tile(TILES - 1)}
+            v_tiles = {}
             q_feat = turn_q(TILES - 1)
             jobs = {}
             for step in range(TILES + 2):
                 t = TILES - 1 - step
-                band_job = jobs.get(t + 1)
-                far_job = jobs.get(t + 2)
-                if far_job is not None:
-                    scale_far(far_job)
+                back_job = jobs.get(t + 1)
+                old_job = jobs.get(t + 2)
+                if old_job is not None:
+                    band_open(old_job)
+                    old_job["to_scale"] = [(s, v_o, h) for s, v_o in old_job["v_far"] for h in range(HEADS)]
+
+                def weave(i):
+                    if i >= HEADS + LAG:
+                        return
+                    if old_job is not None:
+                        band_step(old_job, i)
+                        scale_far(old_job, SCALE_PIECES)
+                    if back_job is not None and i < HEADS and i % SET == SET - 1:
+                        skew_back(back_job["trip"], i // SET)
+
+                woven = 0
                 if t >= 0:
-                    score, unread = scores(t, q_feat)
+                    score, unread, woven = scores(t, q_feat, weave)
+                for i in range(woven, HEADS + LAG):
+                    weave(i)
+                if old_job is not None:
+                    scale_far(old_job, len(old_job["to_scale"]))
+                    band_close(old_job)
                 if t > 0:
                     q_feat = turn_q(t - 1)
-                if far_job is not None:
-                    far_sums(far_job, 0)
+                if t >= 0:
+                    v_tiles[t] = load_v_tile(t)
+                if old_job is not None:
+                    far_sums(old_job, 0)
                 if t >= 0:
                     add_up(score, *unread)
                     u_plus_1, feat = tap_features(t, score, tap_gains[step % 2])
-                if band_job is not None:
-                    band_sums(band_job)
-                if t > 0:
-                    v_tiles[t - 1] = load_v_tile(t - 1)
-                if far_job is not None:
-                    far_sums(far_job, 1)
-                    nc.sync.dma_start(out=out_rows[(t + 2) * P : (t + 3) * P, :], in_=far_job["result"][:])
-                if band_job is not None:
-                    band_job["v_far"] = load_far(t + 1)
+                if old_job is not None:
+                    far_sums(old_job, 1)
+                    nc.sync.dma_start(out=out_rows[(t + 2) * P : (t + 3) * P, :], in_=old_job["result"][:])
+                if back_job is not None:
+                    back_job["v_far"] = load_far(t + 1)
                 if t >= 0:
                     weight = tap_weights(u_plus_1, feat, tap_gains[step % 2])
+                    trip = skew(t, weight)
                     jobs[t] = {
-                        "key_tiles": [0, 1] if t > 0 else [1],
+                        "tile": t,
+                        "key_tiles": trip["key_tiles"],
                         "weight": weight,
-                        "bands": skew(t, weight),
+                        "trip": trip,
+                        "bands": trip["bands"],
                         "bandT": {},
-                        "v_near": {0: v_tiles.get(t - 1), 1: v_tiles[t]},
                     }

@@ -47,6 +47,7 @@ HEAD_SETS = 4
 SET = HEADS // HEAD_SETS
 PITCH = 2 * P
 RAW_AHEAD = 5
+BLOCK_STEPS = 12
 SCALE_PIECES = 6
 GPSIMD_COLUMNS = 2
 LAG = 2
@@ -543,46 +544,53 @@ def tile_dwarfattention_pa_kernel(tc, x, W_qkv, b_qkv, gains, pos_bias, identity
             jobs = {}
             for step in range(TILES + 2):
                 t = TILES - 1 - step
-                back_job = jobs.get(t + 1)
+                new_job = jobs.get(t + 1)
                 old_job = jobs.get(t + 2)
                 if old_job is not None:
-                    band_open(old_job)
                     old_job["to_scale"] = [(s, v_o, h) for s, v_o in old_job["v_far"] for h in range(HEADS)]
 
                 def weave(i):
                     if i >= HEADS + LAG:
                         return
+                    band_i = BLOCK_STEPS + i
                     if old_job is not None:
-                        band_step(old_job, i)
+                        if band_i < HEADS + LAG:
+                            band_step(old_job, band_i)
                         scale_far(old_job, SCALE_PIECES)
-                    if back_job is not None and i < HEADS and i % SET == SET - 1:
-                        skew_back(back_job["trip"], i // SET)
+                    if band_i == HEADS - 1 and new_job is not None:
+                        skew_back(new_job["trip"], HEAD_SETS - 1)
+                    if band_i == HEADS + LAG - 1:
+                        if old_job is not None:
+                            band_close(old_job)
+                        if t >= 0:
+                            v_tiles[t] = load_v_tile(t)
 
                 woven = 0
                 if t >= 0:
                     score, unread, woven = scores(t, q_feat, weave)
                 for i in range(woven, HEADS + LAG):
                     weave(i)
-                if old_job is not None:
-                    scale_far(old_job, len(old_job["to_scale"]))
-                    band_close(old_job)
                 if t > 0:
                     q_feat = turn_q(t - 1)
-                if t >= 0:
-                    v_tiles[t] = load_v_tile(t)
                 if old_job is not None:
                     far_sums(old_job, 0)
                 if t >= 0:
                     add_up(score, *unread)
                     u_plus_1, feat = tap_features(t, score, tap_gains[step % 2])
+                if new_job is not None:
+                    band_open(new_job)
+                    for i in range(BLOCK_STEPS):
+                        band_step(new_job, i)
                 if old_job is not None:
                     far_sums(old_job, 1)
                     nc.sync.dma_start(out=out_rows[(t + 2) * P : (t + 3) * P, :], in_=old_job["result"][:])
-                if back_job is not None:
-                    back_job["v_far"] = load_far(t + 1)
+                if new_job is not None:
+                    new_job["v_far"] = load_far(t + 1)
                 if t >= 0:
                     weight = tap_weights(u_plus_1, feat, tap_gains[step % 2])
                     trip = skew(t, weight)
+                    for hs in range(BLOCK_STEPS // SET):
+                        skew_back(trip, hs)
                     jobs[t] = {
                         "tile": t,
                         "key_tiles": trip["key_tiles"],

@@ -49,6 +49,7 @@ PITCH = 2 * P
 RAW_AHEAD = 5
 BLOCK_STEPS = 12
 SCALE_PIECES = 6
+GPSIMD_PRODUCTS = (1, 4, 6)
 GPSIMD_COLUMNS = 2
 LAG = 2
 
@@ -373,7 +374,7 @@ def tile_dwarfattention_pa_kernel(tc, x, W_qkv, b_qkv, gains, pos_bias, identity
                     for i, s in enumerate(run):
                         first = PAD + t * P - OFFSETS[s]
                         prod = prod_pool.tile([P, GROUPS, P], F32, name="prod")
-                        if unit % 3 == 1:
+                        if unit % 8 in GPSIMD_PRODUCTS:
                             nc.gpsimd.tensor_tensor(
                                 out=prod[:], in0=q_sb[:], in1=k_feat[:, :, first : first + P], op=ALU.mult
                             )

from contextlib import ExitStack

import concourse.mybir as mybir
from concourse.masks import make_identity

F32 = mybir.dt.float32
BF16 = mybir.dt.bfloat16
U32 = mybir.dt.uint32
U8 = mybir.dt.uint8
FP8X4 = mybir.dt.float8_e4m3fn_x4
ALU = mybir.AluOpType
ACT = mybir.ActivationFunctionType
AXIS = mybir.AxisListType

P = 128
TOKENS = 1536
TILES = TOKENS // P
D_IN = 1024
HEADS = 16
HEAD_DIM = 64
E = HEADS * HEAD_DIM
PACK = 4
PASSES = D_IN // (P * PACK)
BANK = 512
BLOCKS = BANK // P
GROUPS = 8
PAD = P

D4 = [0.4829629131445341, 0.8365163037378079, 0.2241438680420134, -0.1294095225512604]
SCALES = 11

POW_SLOT = 1
TRI_SLOT = 12
OFFSETS = [0] + [1 << e for e in range(11)] + [3 << j for j in range(9)]
SLOTS = len(OFFSETS)
BAND = 128
NEAR_SLOTS = [s for s in range(SLOTS) if OFFSETS[s] <= BAND]
FAR_SLOTS = [s for s in range(SLOTS) if OFFSETS[s] > BAND]

LOCAL = 11
TAU1 = 12
TAU2 = 23
TAU3 = 34
ENTRIES = 43

HEAD_SETS = 4
SET = HEADS // HEAD_SETS
PITCH = 2 * P
RAW_AHEAD = 5
BLOCK_STEPS = 12
SCALE_PIECES = 6
GPSIMD_PRODUCTS = (1, 4, 6)
GPSIMD_COLUMNS = 2
LAG = 2

FLOPS = 2 * TOKENS * D_IN * 3 * E + 4 * TOKENS * E * 42


def runs_of_slots(slots, longest):
    runs = []
    for s in slots:
        if runs and runs[-1][-1] == s - 1 and len(runs[-1]) < longest:
            runs[-1].append(s)
        else:
            runs.append([s])
    return runs


def tile_dwarfattention_pa_kernel(tc, x, W_qkv, b_qkv, gains, pos_bias, identity_bypass, out):
    nc = tc.nc
    out_rows = out.rearrange("o n f -> (o n) f")
    out_words = out.rearrange("o n f -> (o n f)")

    with ExitStack() as whole:
        const = whole.enter_context(tc.tile_pool(name="const", bufs=1))
        keep = whole.enter_context(tc.tile_pool(name="keep", bufs=1))

        ident = const.tile([P, P], F32, name="ident")
        make_identity(nc, ident[:])

        q_tok = keep.tile([P, TILES, E], F32, name="q_tok")
        k_feat = keep.tile([P, GROUPS, PAD + TOKENS], F32, name="k_feat")
        nc.vector.memset(k_feat[:, :, 0:PAD], 0.0)

        bias_qk_bf = const.tile([P, 2, GROUPS], BF16, name="bias_qk_bf")
        nc.scalar.dma_start(out=bias_qk_bf[:], in_=b_qkv.rearrange("(s r a) -> r s a", s=3, a=GROUPS)[:, 0:2, :])
        bias_qk = const.tile([P, 2, GROUPS], F32, name="bias_qk")
        nc.vector.tensor_copy(out=bias_qk[:], in_=bias_qk_bf[:])

        pos_bf = const.tile([P, SCALES, 4, HEADS], BF16, name="pos_bf")
        nc.scalar.dma_start(
            out=pos_bf[:].rearrange("p j t h -> p (j t h)"),
            in_=pos_bias.rearrange("r h -> (r h)").partition_broadcast(P),
        )
        bypass_bf = const.tile([P, HEADS], BF16, name="bypass_bf")
        nc.scalar.dma_start(out=bypass_bf[:], in_=identity_bypass.partition_broadcast(P))
        gains_sb = const.tile([P, HEADS, TILES, SCALES], BF16, name="gains_sb")

        bias_plus_1 = const.tile([P, ENTRIES, HEADS], F32, name="bias_plus_1")
        nc.vector.memset(bias_plus_1[:], 1.0)
        for first, tau, j_count in ((0, 0, 11), (TAU1, 1, 11), (TAU2 + 1, 2, 10), (TAU3, 3, 9)):
            nc.vector.tensor_scalar_add(
                out=bias_plus_1[:, first : first + j_count, :], in0=pos_bf[:, 0:j_count, tau, :], scalar1=1.0
            )

        soft = const.tile([P, 3, HEADS], F32, name="soft")
        nc.scalar.activation(out=soft[:, 0, :], in_=bypass_bf[:], func=ACT.Abs)
        nc.scalar.activation(out=soft[:, 1, :], in_=soft[:, 0, :], func=ACT.Exp, scale=-1.0)
        nc.scalar.activation(out=soft[:, 2, :], in_=soft[:, 1, :], func=ACT.Ln, bias=1.0)
        nc.vector.tensor_scalar_max(out=soft[:, 0, :], in0=bypass_bf[:], scalar1=0.0)
        tap_gains = []
        for turn in range(2):
            tap_gain = const.tile([P, ENTRIES, HEADS], F32, name="tap_gain%d" % turn)
            nc.vector.memset(tap_gain[:, TAU2, :], 0.0)
            nc.vector.tensor_tensor(out=tap_gain[:, LOCAL, :], in0=soft[:, 0, :], in1=soft[:, 2, :], op=ALU.add)
            tap_gains.append(tap_gain)

        with ExitStack() as phase:
            raw_pool = phase.enter_context(tc.tile_pool(name="raw", bufs=RAW_AHEAD))
            grouped_pool = phase.enter_context(tc.tile_pool(name="grouped", bufs=2))
            x_pool = phase.enter_context(tc.tile_pool(name="x_mx", bufs=1))
            w_pool = phase.enter_context(tc.tile_pool(name="w_mx", bufs=2))
            v_pool = phase.enter_context(tc.tile_pool(name="v_stage", bufs=3))
            turned_psum = phase.enter_context(tc.psum_pool(name="turned", bufs=4))
            acc_psum = phase.enter_context(tc.psum_pool(name="acc", bufs=4))
            phase.enter_context(tc.manual_schedule())

            bias_v_bf = v_pool.tile([P, E], BF16, name="bias_v_bf", bufs=1)
            nc.scalar.dma_start(out=bias_v_bf[:], in_=b_qkv[2 * E : 3 * E].partition_broadcast(P))
            bias_v = v_pool.tile([P, E], F32, name="bias_v", bufs=1)
            bias_q = v_pool.tile([P, E], F32, name="bias_q", bufs=1)

            x_blocks = x.rearrange("o (n c p) k -> (o n) p c k", c=BLOCKS, p=P)
            w_by_group = W_qkv.rearrange("(s r a) k -> s r a k", s=3, a=GROUPS)
            w_natural = W_qkv.rearrange("(s n c p) k -> s n p c k", s=3, c=BLOCKS, p=P)
            rows_of = {}
            for n in range(TOKENS // BANK):
                rows_of["x%d" % n] = x_blocks[n]
            for n in range(E // BANK):
                rows_of["k%d" % n] = w_by_group[1][:, n * BLOCKS : (n + 1) * BLOCKS, :]
                rows_of["q%d" % n] = w_by_group[0][:, n * BLOCKS : (n + 1) * BLOCKS, :]
                rows_of["v%d" % n] = w_natural[2][n]
            load_order = ["x0", "k0", "x1", "k1", "x2", "q0", "q1", "v0", "v1"]
            raws = {}
            groupeds = {}
            mx = {}

            x_codes = x_pool.tile([P, PASSES, TOKENS], U32, name="x_codes", align_bytes=64)
            x_scales = x_pool.tile([P, PASSES, TOKENS], U8, name="x_scales", align_bytes=64)
            mx["x"] = (x_codes, x_scales)

            def load_next():
                if len(raws) < len(load_order):
                    piece = load_order[len(raws)]
                    raw = raw_pool.tile([P, BLOCKS, D_IN], BF16, name="raw")
                    nc.sync.dma_start(out=raw[:], in_=rows_of[piece])
                    raws[piece] = raw

            def turn(piece):
                raw = raws[piece]
                grouped = grouped_pool.tile([P, PASSES, BANK * PACK], BF16, name="grouped", align_bytes=64)
                grouped_words = grouped[:].bitcast(F32).rearrange("p g (c u) -> p g c u", u=2)
                for c in range(BLOCKS):
                    raw_words = raw[:, c, :].bitcast(F32)
                    turned = turned_psum.tile([P, PASSES, 2, P], F32, name="turned")
                    for g in range(PASSES):
                        for u in range(2):
                            first = (2 * g + u) * P
                            nc.tensor.transpose(turned[:, g, u, :], raw_words[:, first : first + P], ident[:])
                    dst = grouped_words[:, :, c * P : (c + 1) * P, :]
                    src = turned[:].rearrange("p g u c -> p g c u")
                    if c == 1:
                        nc.vector.tensor_copy(out=dst, in_=src)
                    else:
                        nc.scalar.copy(out=dst, in_=src)
                groupeds[piece] = grouped
                load_next()

            def quantise(piece):
                kind, n = piece[0], int(piece[1])
                if kind not in mx:
                    w_codes = w_pool.tile([P, PASSES, E], U32, name="w_codes", align_bytes=64)
                    w_scales = w_pool.tile([P, PASSES, E], U8, name="w_scales", align_bytes=64)
                    mx[kind] = (w_codes, w_scales)
                codes, scales = mx[kind]
                cols = slice(n * BANK, (n + 1) * BANK)
                for g in range(PASSES):
                    nc.vector.quantize_mx(
                        out=codes[:, g, cols].bitcast(FP8X4), scales=scales[:, g, cols], in_=groupeds[piece][:, g, :]
                    )

            def product(lhs, lhs_cols, rhs, rhs_cols):
                acc = acc_psum.tile([P, BANK], F32, name="acc")
                for g in range(PASSES):
                    nc.tensor.matmul_mx(
                        out=acc[:],
                        lhsT=mx[lhs][0][:, g, lhs_cols].bitcast(FP8X4),
                        lhsT_scale=mx[lhs][1][:, g, lhs_cols],
                        rhs=mx[rhs][0][:, g, rhs_cols].bitcast(FP8X4),
                        rhs_scale=mx[rhs][1][:, g, rhs_cols],
                        start=(g == 0),
                        stop=(g == PASSES - 1),
                    )
                return acc

            def project_k(groups, n):
                for a in groups:
                    acc = product("k", slice(a * P, (a + 1) * P), "x", slice(n * BANK, (n + 1) * BANK))
                    dst = k_feat[:, a, PAD + n * BANK : PAD + (n + 1) * BANK]
                    bias = bias_qk[:, 1, a : a + 1]
                    if a % 2 == 0:
                        nc.scalar.activation(out=dst, in_=acc[:], func=ACT.Identity, bias=bias)
                    else:
                        nc.vector.tensor_scalar_add(out=dst, in0=acc[:], scalar1=bias)

            def project_tokens(t, kind, bias_all, dest):
                for n in range(E // BANK):
                    feats = slice(n * BANK, (n + 1) * BANK)
                    acc = product("x", slice(t * P, (t + 1) * P), kind, feats)
                    nc.vector.tensor_tensor(out=dest[:, feats], in0=acc[:], in1=bias_all[:, feats], op=ALU.add)

            def project_q(tiles):
                for t in tiles:
                    project_tokens(t, "q", bias_q, q_tok[:, t, :])

            def spread_bias_q():
                for n in range(E // BANK):
                    acc = acc_psum.tile([P, BANK], F32, name="acc")
                    for c in range(BLOCKS):
                        a = n * BLOCKS + c
                        nc.tensor.matmul(
                            out=acc[:, c * P : (c + 1) * P],
                            lhsT=bias_qk[:, 0, a : a + 1].to_broadcast([P, P]),
                            rhs=ident[:],
                            start=True,
                            stop=True,
                        )
                    nc.scalar.copy(out=bias_q[:, n * BANK : (n + 1) * BANK], in_=acc[:])

            lower, upper = range(0, BLOCKS), range(BLOCKS, GROUPS)
            for i in range(RAW_AHEAD):
                load_next()
            turn("x0")
            turn("k0")
            quantise("x0")
            turn("x1")
            quantise("k0")
            spread_bias_q()
            turn("k1")
            quantise("x1")
            project_k(lower, 0)
            turn("x2")
            quantise("k1")
            project_k(lower, 1)
            turn("q0")
            quantise("x2")
            project_k(upper, 0)
            project_k(upper, 1)
            turn("q1")
            quantise("q0")
            project_k(lower, 2)
            quantise("q1")
            nc.vector.tensor_copy(out=bias_v[:], in_=bias_v_bf[:])
            project_k(upper, 2)
            nc.sync.dma_start(
                out=gains_sb[:].rearrange("p h t j -> p (h t) j"),
                in_=gains.rearrange("o h (t p) j -> p (o h t) j", p=P),
            )
            project_q(range(0, 3))
            turn("v0")
            project_q(range(3, 6))
            quantise("v0")
            turn("v1")
            project_q(range(6, 9))
            quantise("v1")
            project_q(range(9, TILES))
            for t in range(TILES):
                v_stage = v_pool.tile([P, E], F32, name="v_stage")
                project_tokens(t, "v", bias_v, v_stage)
                nc.sync.dma_start(out=out_rows[t * P : (t + 1) * P, :], in_=v_stage[:])

        with ExitStack() as phase:
            prod_pool = phase.enter_context(tc.tile_pool(name="prod", bufs=6))
            mid_pool = phase.enter_context(tc.tile_pool(name="mid", bufs=1))
            lag_pool = phase.enter_context(tc.tile_pool(name="lag", bufs=2))
            band_pool = phase.enter_context(tc.tile_pool(name="band", bufs=2 * HEAD_SETS))
            bandT_pool = phase.enter_context(tc.tile_pool(name="bandT", bufs=4))
            near_pool = phase.enter_context(tc.tile_pool(name="v_near", bufs=2))
            far_pool = phase.enter_context(tc.tile_pool(name="v_far", bufs=len(FAR_SLOTS)))
            score_psum = phase.enter_context(tc.psum_pool(name="score", bufs=2))
            bandT_psum = phase.enter_context(tc.psum_pool(name="bandT_ps", bufs=2))
            sum_psum = phase.enter_context(tc.psum_pool(name="sum", bufs=1))
            q_psum = phase.enter_context(tc.psum_pool(name="q", bufs=1))
            phase.enter_context(tc.manual_schedule())

            band_rows = mid_pool.tile([P, HEADS, PITCH], F32, name="band_rows")
            nc.vector.memset(band_rows[:], 0.0)

            def load_v_tile(t):
                v_near = near_pool.tile([P, E], F32, name="v_near")
                nc.scalar.dma_start(out=v_near[:], in_=out_rows[t * P : (t + 1) * P, :])
                return v_near

            def sum_cols(job, h):
                first = h * HEAD_DIM % BANK
                return job["sums"][h * HEAD_DIM // BANK][:, first : first + HEAD_DIM]

            def band_open(job):
                job["sums"] = [sum_psum.tile([P, BANK], F32, name="sum%d" % n) for n in range(E // BANK)]

            def band_close(job):
                job["result"] = lag_pool.tile([P, E], F32, name="result")
                for n in range(E // BANK):
                    nc.scalar.copy(out=job["result"][:, n * BANK : (n + 1) * BANK], in_=job["sums"][n][:])

            def band_step(job, i):
                key_tiles = job["key_tiles"]
                if i < HEADS:
                    bandT_ps = bandT_psum.tile([P, 2, P], F32, name="bandT_ps")
                    for kt in key_tiles:
                        nc.tensor.transpose(bandT_ps[:, kt, :], job["bands"][i // SET][kt][:, i % SET, :], ident[:])
                    bandT = bandT_pool.tile([P, 2, P], F32, name="bandT")
                    nc.scalar.copy(out=bandT[:, key_tiles[0] : 2, :], in_=bandT_ps[:, key_tiles[0] : 2, :])
                    job["bandT"][i] = bandT
                h = i - LAG
                if h >= 0:
                    for kt in key_tiles:
                        nc.tensor.matmul(
                            out=sum_cols(job, h),
                            lhsT=job["bandT"][h][:, kt, :],
                            rhs=v_tiles[job["tile"] - 1 + kt][:, h * HEAD_DIM : (h + 1) * HEAD_DIM],
                            start=(kt == key_tiles[0]),
                            stop=(kt == key_tiles[-1]),
                        )

            def add_up(score, partial, run):
                nc.vector.tensor_reduce(
                    out=score[:, run[0] : run[0] + len(run), :],
                    in_=partial[:, 0 : len(run), :].rearrange("p s (h b) -> p s h b", b=GROUPS),
                    axis=AXIS.X,
                    op=ALU.add,
                )

            def turn_and_add(partial, i, prod, groups):
                for a in range(groups):
                    nc.tensor.matmul(
                        out=partial[:, i, :],
                        lhsT=prod[:, a, :],
                        rhs=ident[:],
                        is_transpose=True,
                        start=(a == 0),
                        stop=(a == groups - 1),
                    )

            def turn_q(t):
                q_feat = [q_psum.tile([P, BLOCKS, P], F32, name="q_feat%d" % n) for n in range(GROUPS // BLOCKS)]
                for a in range(GROUPS):
                    nc.tensor.transpose(q_feat[a // BLOCKS][:, a % BLOCKS, :], q_tok[:, t, a * P : (a + 1) * P], ident[:])
                q_sb = mid_pool.tile([P, GROUPS, P], F32, name="q_sb")
                for n in range(GROUPS // BLOCKS):
                    nc.scalar.copy(out=q_sb[:, n * BLOCKS : (n + 1) * BLOCKS, :], in_=q_feat[n][:])
                return q_feat, q_sb

            def scores(t, q_pair, weave):
                score = lag_pool.tile([P, SLOTS, HEADS], F32, name="score", bufs=1)
                live = [s for s in range(SLOTS) if OFFSETS[s] < (t + 1) * P]
                if len(live) < SLOTS:
                    nc.vector.memset(score[:], 0.0)
                q_feat, q_sb = q_pair
                unread = None
                unit = 0
                for run in runs_of_slots(live, BLOCKS):
                    partial = score_psum.tile([P, BLOCKS, P], F32, name="partial")
                    for i, s in enumerate(run):
                        first = PAD + t * P - OFFSETS[s]
                        prod = prod_pool.tile([P, GROUPS, P], F32, name="prod")
                        if unit % 8 in GPSIMD_PRODUCTS:
                            nc.gpsimd.tensor_tensor(
                                out=prod[:], in0=q_sb[:], in1=k_feat[:, :, first : first + P], op=ALU.mult
                            )
                        else:
                            for n in range(GROUPS // BLOCKS):
                                groups = slice(n * BLOCKS, (n + 1) * BLOCKS)
                                nc.vector.tensor_tensor(
                                    out=prod[:, groups, :],
                                    in0=q_feat[n][:],
                                    in1=k_feat[:, groups, first : first + P],
                                    op=ALU.mult,
                                )
                        if unread is not None and i == len(run) - 1:
                            add_up(score, *unread)
                            unread = None
                        turn_and_add(partial, i, prod, GROUPS)
                        weave(unit)
                        unit += 1
                    unread = (partial, run)
                return score, unread, unit

            def tap_features(t, score, tap_gain):
                g_jh = gains_sb[:, :, t, :].rearrange("p h j -> p j h")
                nc.scalar.mul(out=tap_gain[:, 0:11, :], in_=g_jh, mul=D4[0])
                nc.scalar.mul(out=tap_gain[:, TAU1 : TAU1 + 11, :], in_=g_jh, mul=D4[1])
                nc.scalar.mul(out=tap_gain[:, TAU2 + 1 : TAU2 + 11, :], in_=g_jh[:, 0:10, :], mul=D4[2])
                nc.scalar.mul(out=tap_gain[:, TAU3 : TAU3 + 9, :], in_=g_jh[:, 0:9, :], mul=abs(D4[3]))

                u_plus_1 = mid_pool.tile([P, ENTRIES, HEADS], F32, name="u_plus_1")
                nc.vector.tensor_tensor(
                    out=u_plus_1[:, 0:TAU1, :],
                    in0=score[:, 0:1, :].to_broadcast([P, TAU1, HEADS]),
                    in1=bias_plus_1[:, 0:TAU1, :],
                    op=ALU.add,
                )
                nc.vector.tensor_tensor(
                    out=u_plus_1[:, TAU1:TAU3, :].rearrange("p (b s) h -> p b (s h)", b=2),
                    in0=score[:, POW_SLOT:TRI_SLOT, :]
                    .rearrange("p s h -> p (s h)")
                    .unsqueeze(1)
                    .to_broadcast([P, 2, 11 * HEADS]),
                    in1=bias_plus_1[:, TAU1:TAU3, :].rearrange("p (b s) h -> p b (s h)", b=2),
                    op=ALU.add,
                )
                nc.vector.tensor_tensor(
                    out=u_plus_1[:, TAU3:ENTRIES, :],
                    in0=score[:, TRI_SLOT:SLOTS, :],
                    in1=bias_plus_1[:, TAU3:ENTRIES, :],
                    op=ALU.add,
                )
                feat = mid_pool.tile([P, ENTRIES, HEADS], F32, name="feat")
                nc.scalar.activation(
                    out=feat[:].rearrange("p e h -> p (e h)"),
                    in_=u_plus_1[:].rearrange("p e h -> p (e h)"),
                    func=ACT.Exp,
                    bias=-1.0,
                )
                return u_plus_1, feat

            def tap_weights(u_plus_1, feat, tap_gain):
                feat_flat = feat[:].rearrange("p e h -> p (e h)")
                nc.vector.scalar_tensor_tensor(
                    out=feat_flat,
                    in0=feat_flat,
                    scalar=1.0,
                    in1=u_plus_1[:].rearrange("p e h -> p (e h)"),
                    op0=ALU.min,
                    op1=ALU.max,
                )
                tap_mass = mid_pool.tile([P, TAU3, HEADS], F32, name="tap_mass")
                mass = mid_pool.tile([P, SLOTS, HEADS], F32, name="mass")
                nc.vector.tensor_tensor(out=tap_mass[:], in0=feat[:, 0:TAU3, :], in1=tap_gain[:, 0:TAU3, :], op=ALU.mult)
                nc.vector.tensor_tensor(
                    out=mass[:, TRI_SLOT:SLOTS, :], in0=feat[:, TAU3:ENTRIES, :], in1=tap_gain[:, TAU3:ENTRIES, :], op=ALU.mult
                )
                nc.vector.tensor_reduce(
                    out=mass[:, 0, :], in_=tap_mass[:, 0:TAU1, :].rearrange("p e h -> p h e"), axis=AXIS.X, op=ALU.add
                )
                nc.vector.tensor_tensor(
                    out=mass[:, POW_SLOT:TRI_SLOT, :], in0=tap_mass[:, TAU1:TAU2, :], in1=tap_mass[:, TAU2:TAU3, :], op=ALU.add
                )
                z = mid_pool.tile([P, HEADS], F32, name="z")
                nc.vector.tensor_reduce(out=z[:], in_=mass[:].rearrange("p s h -> p h s"), axis=AXIS.X, op=ALU.add)
                nc.vector.tensor_scalar_add(out=z[:], in0=z[:], scalar1=1e-6)
                nc.vector.reciprocal(out=z[:], in_=z[:])
                weight = lag_pool.tile([P, SLOTS, HEADS], F32, name="weight")
                nc.vector.tensor_tensor(
                    out=weight[:, 0:TRI_SLOT, :],
                    in0=mass[:, 0:TRI_SLOT, :],
                    in1=z[:].unsqueeze(1).to_broadcast([P, TRI_SLOT, HEADS]),
                    op=ALU.mult,
                )
                nc.vector.scalar_tensor_tensor(
                    out=weight[:, TRI_SLOT:SLOTS, :],
                    in0=mass[:, TRI_SLOT:SLOTS, :],
                    scalar=-1.0,
                    in1=z[:].unsqueeze(1).to_broadcast([P, SLOTS - TRI_SLOT, HEADS]),
                    op0=ALU.mult,
                    op1=ALU.mult,
                )
                return weight

            def skew(t, weight):
                for s in NEAR_SLOTS[:-GPSIMD_COLUMNS]:
                    nc.vector.tensor_copy(out=band_rows[:, :, BAND - OFFSETS[s]], in_=weight[:, s, :])
                for s in NEAR_SLOTS[-GPSIMD_COLUMNS:]:
                    nc.gpsimd.tensor_copy(out=band_rows[:, :, BAND - OFFSETS[s]], in_=weight[:, s, :])
                free_tiles = [t, t + 1] if t + 1 < TILES else [t]
                trip = {"free_tiles": free_tiles, "key_tiles": [0, 1] if t > 0 else [1], "bands": []}
                for hs in range(len(free_tiles)):
                    skew_out(trip, hs)
                return trip

            def skew_words(trip, hs):
                r = trip["free_tiles"][hs % len(trip["free_tiles"])]
                return out_words[r * P * E : (r + 1) * P * E]

            def skew_out(trip, hs):
                nc.sync.dma_start(
                    out=skew_words(trip, hs).rearrange("(h n c) -> n h c", h=SET, c=PITCH),
                    in_=band_rows[:, hs * SET : (hs + 1) * SET, :],
                )

            def skew_back(trip, hs):
                by_head = skew_words(trip, hs).rearrange("(h w) -> h w", h=SET)
                band = {}
                for kt in trip["key_tiles"]:
                    band[kt] = band_pool.tile([P, SET, P], F32, name="band")
                    nc.sync.dma_start(
                        out=band[kt][:],
                        in_=by_head[:, kt * P : kt * P + P * (PITCH - 1)].rearrange("h (n c) -> n h c", c=PITCH - 1)[
                            :, :, 0:P
                        ],
                    )
                trip["bands"].append(band)
                if hs + len(trip["free_tiles"]) < HEAD_SETS:
                    skew_out(trip, hs + len(trip["free_tiles"]))

            def load_far(t):
                tiles = []
                for s in FAR_SLOTS:
                    first = t * P - OFFSETS[s]
                    if first + P <= 0:
                        continue
                    v_far = far_pool.tile([P, E], F32, name="v_far")
                    missing = max(0, -first)
                    if missing:
                        nc.vector.memset(v_far[0:missing, :], 0.0)
                    nc.sync.dma_start(out=v_far[missing:P, :], in_=out_rows[first + missing : first + P, :])
                    tiles.append((s, v_far))
                return tiles

            def scale_far(job, count):
                for s, v_o, h in job["to_scale"][:count]:
                    cols = slice(h * HEAD_DIM, (h + 1) * HEAD_DIM)
                    nc.scalar.activation(
                        out=v_o[:, cols], in_=v_o[:, cols], func=ACT.Copy, scale=job["weight"][:, s, h : h + 1]
                    )
                job["to_scale"] = job["to_scale"][count:]

            def far_sums(job, part):
                result = job["result"]
                for s, v_o in job["v_far"][part::2]:
                    nc.vector.tensor_tensor(out=result[:], in0=result[:], in1=v_o[:], op=ALU.add)

            v_tiles = {}
            q_feat = turn_q(TILES - 1)
            jobs = {}
            for step in range(TILES + 2):
                t = TILES - 1 - step
                new_job = jobs.get(t + 1)
                old_job = jobs.get(t + 2)
                if old_job is not None:
                    old_job["to_scale"] = [(s, v_o, h) for s, v_o in old_job["v_far"] for h in range(HEADS)]

                def weave(i):
                    if i >= HEADS + LAG:
                        return
                    band_i = BLOCK_STEPS + i
                    if old_job is not None:
                        if band_i < HEADS + LAG:
                            band_step(old_job, band_i)
                        scale_far(old_job, SCALE_PIECES)
                    if band_i == HEADS - 1 and new_job is not None:
                        skew_back(new_job["trip"], HEAD_SETS - 1)
                    if band_i == HEADS + LAG - 1:
                        if old_job is not None:
                            band_close(old_job)
                        if t >= 0:
                            v_tiles[t] = load_v_tile(t)

                woven = 0
                if t >= 0:
                    score, unread, woven = scores(t, q_feat, weave)
                for i in range(woven, HEADS + LAG):
                    weave(i)
                if t > 0:
                    q_feat = turn_q(t - 1)
                if old_job is not None:
                    far_sums(old_job, 0)
                if t >= 0:
                    add_up(score, *unread)
                    u_plus_1, feat = tap_features(t, score, tap_gains[step % 2])
                if new_job is not None:
                    band_open(new_job)
                    for i in range(BLOCK_STEPS):
                        band_step(new_job, i)
                if old_job is not None:
                    far_sums(old_job, 1)
                    nc.sync.dma_start(out=out_rows[(t + 2) * P : (t + 3) * P, :], in_=old_job["result"][:])
                if new_job is not None:
                    new_job["v_far"] = load_far(t + 1)
                if t >= 0:
                    weight = tap_weights(u_plus_1, feat, tap_gains[step % 2])
                    trip = skew(t, weight)
                    for hs in range(BLOCK_STEPS // SET):
                        skew_back(trip, hs)
                    jobs[t] = {
                        "tile": t,
                        "key_tiles": trip["key_tiles"],
                        "weight": weight,
                        "trip": trip,
                        "bands": trip["bands"],
                        "bandT": {},
                    }
